import numpy as np
import ml_dtypes


def mxq(x, axis, fmt="e4m3"):
    dtype, down = {"e4m3": (ml_dtypes.float8_e4m3fn, 7), "e5m2": (ml_dtypes.float8_e5m2, 14)}[fmt]
    v = np.moveaxis(np.asarray(x, np.float32).astype(ml_dtypes.bfloat16).astype(np.float64), axis, -1)
    blocks = v.reshape(v.shape[:-1] + (-1, 32))
    amax = np.abs(blocks).max(-1, keepdims=True)
    byte = np.maximum(np.where(amax > 0, np.frexp(amax)[1] - 1 + 127, 0) - down, 1)
    scale = np.exp2(byte - 127.0)
    codes = (blocks / scale).astype(np.float32).astype(dtype).astype(np.float64)
    return np.moveaxis((codes * scale).reshape(v.shape), -1, axis)


WIDE = False


def mx_kscale(k):
    if not WIDE:
        return np.ones(k)
    levels = np.array([10, -10, 5, -5, 0])
    if k % 512:
        return np.exp2(np.random.permutation(np.resize(levels, k // 32))).repeat(32)
    a = np.empty((k // 512, 16))
    for p in range(k // 512):
        a[p, :8] = np.random.permutation(np.resize(levels, 8))
        for g in range(8):
            far = levels[np.abs(levels - a[p, g]) >= 10]
            a[p, g + 8] = far[np.random.randint(len(far))]
    return np.exp2(a.ravel()).repeat(32)


BF16 = ml_dtypes.bfloat16


def bf(x):
    return np.asarray(x, np.float32).astype(BF16)


def f64(x):
    return np.asarray(x).astype(np.float64)


N, IN_CH, OUT_CH = 4096, 128, 128


def setup_inputs():
    t = mx_kscale(N)
    w = t.max() / t
    g = w.mean()
    a = 1.0 / (1.0 + N * np.random.random((N, N)))
    return {"x": bf(np.random.standard_normal((N, IN_CH)) * 2.0 * (g / w)[:, None]),
            "edge_index": bf(a * w),
            "weight": bf(np.random.standard_normal((IN_CH, OUT_CH)) * 2.0 / np.sqrt(IN_CH)),
            "bias": bf(np.random.standard_normal(OUT_CH) * 0.2)}


def reference(x, edge_index, weight, bias):
    adj = f64(edge_index) + np.eye(edge_index.shape[0])
    adj_sq = np.square(adj)
    row_sum = adj.sum(axis=-1)
    denom = np.square(row_sum) - adj_sq.sum(axis=-1)
    with np.errstate(divide="ignore"):
        norm = 1.0 / denom
    norm = np.where(np.isinf(norm), 0.0, norm)
    xw = f64(x) @ f64(weight)
    s = mxq(adj, 1, "e4m3") @ mxq(xw, 0, "e4m3")
    out = np.square(s) - (mxq(adj_sq, 1, "e4m3") @ mxq(np.square(xw), 0, "e4m3"))
    return norm[:, None] * out + f64(bias)

@@ -1,0 +1,410 @@
+from contextlib import ExitStack
+
+import concourse.mybir as mybir
+from concourse.masks import make_identity
+
+F32 = mybir.dt.float32
+BF16 = mybir.dt.bfloat16
+U32 = mybir.dt.uint32
+U8 = mybir.dt.uint8
+FP8X4 = mybir.dt.float8_e4m3fn_x4
+ALU = mybir.AluOpType
+ACT = mybir.ActivationFunctionType
+AX = mybir.AxisListType
+
+P = 128
+N = 4096
+C = 128
+NT = N // P
+PASS = 512
+NG = N // PASS
+BANK = 512
+HALF = N // 2
+FLOPS = 2 * N * N * C * 2 + 2 * N * C * C
+
+GRAM_STEP = 8
+GRAM_TILES = (3, 11, 19, 27)
+E_BUFS = 6
+H_FIRST = 2
+H_TAIL = 2
+ROUND_1 = NT - 4
+
+
+def tile_bgnna_kernel(tc, x, edge_index, weight, bias, out):
+    nc = tc.nc
+    with ExitStack() as ctx:
+        const = ctx.enter_context(tc.tile_pool(name="const", bufs=1))
+        epool = ctx.enter_context(tc.tile_pool(name="epool", bufs=E_BUFS))
+        gpool = ctx.enter_context(tc.tile_pool(name="gpool", bufs=3))
+        cpool = ctx.enter_context(tc.tile_pool(name="cpool", bufs=3))
+        work = ctx.enter_context(tc.tile_pool(name="work", bufs=2))
+        tpsum = ctx.enter_context(tc.psum_pool(name="tpsum", bufs=5))
+        apsum = ctx.enter_context(tc.psum_pool(name="apsum", bufs=1))
+        ctx.enter_context(tc.manual_schedule())
+
+        e_tiles = {}
+
+        def load(t, pieces):
+            e_t = epool.tile([P, N], BF16, name="e_t")
+            e_tiles[t] = e_t
+            w = N // pieces
+            for k in range(pieces):
+                nc.sync.dma_start(out=e_t[:, w * k : w * k + w], in_=edge_index[t * P : (t + 1) * P, w * k : w * k + w])
+
+        load(0, 4)
+        x_sb = const.tile([P, N], BF16)
+        nc.sync.dma_start(
+            out=x_sb[:].rearrange("q (g r) -> q g r", g=NG),
+            in_=x.rearrange("(g q t) i -> q g (t i)", g=NG, q=P, t=4),
+        )
+        w_sb = const.tile([P, C], BF16)
+        nc.sync.dma_start(out=w_sb[:], in_=weight)
+        load(1, 1)
+        load(2, 1)
+        load(3, 1)
+        bias_bc = const.tile([P, C], BF16)
+        nc.sync.dma_start(out=bias_bc[:], in_=bias.partition_broadcast(P))
+        diag_b = const.tile([P, NT], BF16)
+        with nc.allow_non_contiguous_dma(reason="the 4096 diagonal elements, one each"):
+            nc.sync.dma_start(
+                out=diag_b[:],
+                in_=edge_index.rearrange("a b -> (a b)")[0 : N * N : N + 1].rearrange("(t p) -> p t", p=P),
+            )
+
+        ident_f = const.tile([P, P], F32)
+        make_identity(nc, ident_f[:])
+        sq_sums = const.tile([P, 2 * NT], F32)
+        nc.gpsimd.memset(sq_sums[:], 0.0)
+        fold = const.tile([P, 4, P], F32)
+        nc.gpsimd.memset(fold[:], 0.0)
+        mask = const.tile([P, 4, PASS], BF16)
+        nc.vector.memset(mask[:], 0.0)
+        ident_b = const.tile([P, P], BF16)
+        nc.vector.tensor_copy(out=ident_b[:], in_=ident_f[:])
+        ones_b = const.tile([P, 2], BF16)
+        nc.vector.memset(ones_b[:], 1.0)
+
+        def build_mask(v):
+            view = mask[:, v, :].rearrange("p (h a t) -> p h a t", h=P // 4, a=4, t=4)
+            for a in range(4):
+                nc.vector.tensor_copy(out=view[:, :, a, a], in_=ident_b[:, 32 * v : 32 * v + 32])
+
+        def build_fold():
+            quarter = const.tile([P, 32], F32)
+            nc.vector.tensor_reduce(out=quarter[:], in_=ident_f[:].rearrange("p (c t) -> p c t", t=4), axis=AX.X, op=ALU.add)
+            for s in range(4):
+                nc.vector.tensor_copy(out=fold[:, s, 32 * s : 32 * s + 32], in_=quarter[:])
+
+        scrap = const.tile([P, N], BF16)
+        result = const.tile([P, NT * C], F32)
+        row_part = apsum.tile([P, 4 * NT], F32)
+        gram_part = const.tile([P, 4 * len(GRAM_TILES)], F32)
+        banks = {}
+        grouped = {}
+        exact = {}
+        codes = {}
+        grams = {}
+        products = {}
+        squared = {}
+
+        halves = [(t, k) for t in range(NT) if t not in GRAM_TILES for k in range(2)]
+        progress = {"halves": 0, "loads": 4}
+
+        def square_halves(upto):
+            while progress["halves"] < upto:
+                t, k = halves[progress["halves"]]
+                cols = slice(HALF * k, HALF * k + HALF)
+                nc.scalar.activation(
+                    out=scrap[:, cols], in_=e_tiles[t][:, cols], func=ACT.Square, accum_out=sq_sums[:, 2 * t + k : 2 * t + k + 1]
+                )
+                progress["halves"] += 1
+
+        def more_loads(transposed):
+            while progress["loads"] < NT:
+                old = progress["loads"] - E_BUFS
+                if old > transposed:
+                    return
+                if old >= 0 and old not in GRAM_TILES and halves.index((old, 1)) >= progress["halves"]:
+                    return
+                load(progress["loads"], 1)
+                progress["loads"] += 1
+
+        def bank_order(t):
+            first = (t // 4) // 2
+            return [first] + [h for h in range(4) if h != first]
+
+        def transposes(t):
+            words = e_tiles[t][:].bitcast(F32)
+            for h in bank_order(t):
+                tp = tpsum.tile([P, BANK], F32, tag="tp")
+                banks[(t, h)] = tp
+                for k in range(4):
+                    g, u = 2 * h + k // 2, k % 2
+                    nc.tensor.transpose(out=tp[:, P * k : P * k + P], in_=words[:, 256 * g + u : 256 * (g + 1) : 2], identity=ident_f[:])
+
+        def new_grouped(t):
+            adj_g = gpool.tile([P, N], BF16, name="adj_g", align_bytes=64)
+            sq_g = gpool.tile([P, N], BF16, name="sq_g", align_bytes=64)
+            grouped[t] = (adj_g, sq_g)
+
+        def copy_bank(t, h, engine_copy):
+            engine_copy(
+                out=grouped[t][0][:].bitcast(F32)[:, BANK * h : BANK * h + BANK].rearrange("p (g i u) -> p g i u", g=2, i=P, u=2),
+                in_=banks[(t, h)][:].rearrange("p (g u i) -> p g i u", g=2, u=2, i=P),
+            )
+
+        def diagonal_bank(t):
+            g_d = t // 4
+            tp = banks[(t, g_d // 2)]
+            at = 256 * (g_d % 2)
+            other = 256 - at
+            adj_x = work.tile([P, PASS], F32, name="adj_x")
+            exact[t] = adj_x
+            nc.vector.tensor_tensor(
+                out=adj_x[:].rearrange("p (i u e) -> p i u e", i=P, u=2, e=2),
+                in0=tp[:].bitcast(BF16)[:, 2 * at : 2 * at + PASS].rearrange("p (u i e) -> p i u e", u=2, i=P, e=2),
+                in1=mask[:, t % 4, :].rearrange("p (i u e) -> p i u e", i=P, u=2, e=2),
+                op=ALU.add,
+            )
+            w0 = BANK * (g_d // 2) + other
+            nc.vector.tensor_copy(
+                out=grouped[t][0][:].bitcast(F32)[:, w0 : w0 + 256].rearrange("p (i u) -> p i u", i=P, u=2),
+                in_=tp[:, other : other + 256].rearrange("p (u i) -> p i u", u=2, i=P),
+            )
+
+        def diagonal_adj(t):
+            nc.vector.tensor_copy(out=grouped[t][0][:, PASS * (t // 4) : PASS * (t // 4) + PASS], in_=exact[t][:])
+
+        def diagonal_sq(t):
+            nc.scalar.activation(out=grouped[t][1][:, PASS * (t // 4) : PASS * (t // 4) + PASS], in_=exact[t][:], func=ACT.Square)
+
+        def squares(t):
+            adj_g, sq_g = grouped[t]
+            for lo, hi in ((0, PASS * (t // 4)), (PASS * (t // 4) + PASS, N)):
+                if hi > lo:
+                    nc.vector.tensor_tensor(out=sq_g[:, lo:hi], in0=adj_g[:, lo:hi], in1=adj_g[:, lo:hi], op=ALU.mult)
+
+        def new_codes(t):
+            a_c = cpool.tile([P, N // 4], U32, name="a_c", align_bytes=64)
+            a_s = cpool.tile([P, N // 4], U8, name="a_s", align_bytes=64)
+            s_c = cpool.tile([P, N // 4], U32, name="s_c", align_bytes=64)
+            s_s = cpool.tile([P, N // 4], U8, name="s_s", align_bytes=64)
+            codes[t] = ((a_c, a_s), (s_c, s_s))
+
+        def quantise(t, which):
+            words, scales = codes[t][which]
+            nc.vector.quantize_mx(out=words[:].bitcast(FP8X4), scales=scales[:], in_=grouped[t][which][:])
+
+        def row_sums(t):
+            adj_g = grouped[t][0]
+            for s in range(4):
+                for g in range(NG):
+                    c0 = PASS * g + P * s
+                    nc.tensor.matmul(
+                        out=row_part[:, 4 * t + s : 4 * t + s + 1], lhsT=adj_g[:, c0 : c0 + P], rhs=ones_b[:, 0:1], start=(g == 0), stop=(g == NG - 1)
+                    )
+
+        def gram(t):
+            adj_g = grouped[t][0]
+            gr = tpsum.tile([P, BANK], F32, tag="tp")
+            grams[t] = gr
+            for s in range(4):
+                for g in range(NG):
+                    c0 = PASS * g + P * s
+                    nc.tensor.matmul(
+                        out=gr[:, P * s : P * s + P], lhsT=adj_g[:, c0 : c0 + P], rhs=adj_g[:, c0 : c0 + P], start=(g == 0), stop=(g == NG - 1)
+                    )
+
+        def gram_diagonal(t):
+            kept = work.tile([P, BANK], F32, name="kept")
+            nc.vector.tensor_tensor(
+                out=kept[:].rearrange("p (s m) -> p s m", s=4),
+                in0=grams[t][:].rearrange("p (s m) -> p s m", s=4),
+                in1=ident_f[:].unsqueeze(1).to_broadcast([P, 4, P]),
+                op=ALU.mult,
+            )
+            at = 4 * GRAM_TILES.index(t)
+            nc.vector.tensor_reduce(out=gram_part[:, at : at + 4], in_=kept[:].rearrange("p (s m) -> p s m", s=4), axis=AX.X, op=ALU.add)
+
+        xw_codes = []
+
+        def mx(t):
+            if t % 4 == 0:
+                s_ps = apsum.tile([P, BANK], F32, name="s_ps")
+                q_ps = apsum.tile([P, BANK], F32, name="q_ps")
+                products[t // 4] = (s_ps, q_ps)
+            for which in range(2):
+                l_c, l_s = codes[t][which]
+                r_c, r_s = xw_codes[which]
+                for g in range(NG):
+                    cols = slice(P * g, P * g + P)
+                    nc.tensor.matmul_mx(
+                        out=products[t // 4][which][:, P * (t % 4) : P * (t % 4) + P],
+                        lhsT=l_c[:, cols].bitcast(FP8X4),
+                        lhsT_scale=l_s[:, cols],
+                        rhs=r_c[:, cols].bitcast(FP8X4),
+                        rhs_scale=r_s[:, cols],
+                        start=(g == 0),
+                        stop=(g == NG - 1),
+                    )
+
+        def square_s(b):
+            s2 = work.tile([P, BANK], F32, name="s2")
+            squared[b] = s2
+            nc.scalar.activation(out=s2[:], in_=products[b][0][:], func=ACT.Square)
+
+        def minus_q(b):
+            nc.vector.tensor_tensor(out=result[:, BANK * b : BANK * b + BANK], in0=squared[b][:], in1=products[b][1][:], op=ALU.subtract)
+
+        xt_sb = const.tile([P, N], BF16)
+        xw_g = const.tile([P, N], BF16, align_bytes=64)
+        xw2_g = const.tile([P, N], BF16, align_bytes=64)
+
+        def x_transposed():
+            for k in range(4):
+                xtp = tpsum.tile([P, 2 * BANK], BF16, tag="tp")
+                for j in range(8):
+                    b = 8 * k + j
+                    nc.tensor.transpose(out=xtp[:, P * j : P * j + P], in_=x_sb[:, P * b : P * b + P], identity=ident_b[:])
+                nc.scalar.copy(out=xt_sb[:, 1024 * k : 1024 * k + 1024], in_=xtp[:])
+
+        def xw_quantised():
+            for g in range(NG):
+                xwp = tpsum.tile([P, BANK], F32, tag="tp")
+                for t in range(4):
+                    b = 4 * g + t
+                    nc.tensor.matmul(out=xwp[:, P * t : P * t + P], lhsT=xt_sb[:, P * b : P * b + P], rhs=w_sb[:], start=True, stop=True)
+                cols = slice(PASS * g, PASS * g + PASS)
+                nc.vector.tensor_copy(out=xw_g[:, cols].rearrange("p (c t) -> p c t", t=4), in_=xwp[:].rearrange("p (t c) -> p c t", t=4))
+                nc.scalar.activation(
+                    out=xw2_g[:, cols].rearrange("p (c t) -> p c t", t=4), in_=xwp[:].rearrange("p (t c) -> p c t", t=4), func=ACT.Square
+                )
+            for name, src in (("xw", xw_g), ("xw2", xw2_g)):
+                words = const.tile([P, N // 4], U32, name=name + "_c", align_bytes=64)
+                scales = const.tile([P, N // 4], U8, name=name + "_s", align_bytes=64)
+                xw_codes.append((words, scales))
+                nc.vector.quantize_mx(out=words[:].bitcast(FP8X4), scales=scales[:], in_=src[:])
+
+        small = {}
+        for name in ("diag", "one_d", "rest", "extra", "sq_x", "sq_r", "rows", "rows2", "ss_a", "ss_b", "ss_c", "den", "nz", "pad", "safe", "rec", "norm"):
+            small[name] = const.tile([P, NT], F32, name=name)
+        one_d_b = const.tile([P, NT], BF16)
+
+        def diagonal_terms():
+            gt = slice(GRAM_TILES[0], NT, GRAM_STEP)
+            nc.vector.tensor_copy(out=small["diag"][:], in_=diag_b[:])
+            nc.vector.tensor_scalar_add(out=small["one_d"][:], in0=small["diag"][:], scalar1=1.0)
+            nc.vector.tensor_copy(out=one_d_b[:], in_=small["one_d"][:])
+            nc.vector.tensor_tensor(out=small["rest"][:], in0=small["one_d"][:], in1=one_d_b[:], op=ALU.subtract)
+            nc.vector.tensor_scalar(out=small["extra"][:], in0=small["diag"][:], scalar1=2.0, scalar2=1.0, op0=ALU.mult, op1=ALU.add)
+            nc.vector.tensor_tensor(out=small["sq_x"][:], in0=small["one_d"][:], in1=small["one_d"][:], op=ALU.mult)
+            nc.vector.tensor_tensor(out=small["sq_r"][:], in0=one_d_b[:], in1=one_d_b[:], op=ALU.mult)
+            nc.vector.tensor_tensor(out=small["extra"][:, gt], in0=small["sq_x"][:, gt], in1=small["sq_r"][:, gt], op=ALU.subtract)
+
+        row_sb = const.tile([P, 4 * NT], F32)
+        folded = {}
+
+        def fold_sums(lo, hi):
+            nc.vector.tensor_copy(out=row_sb[:, 4 * lo : 4 * hi], in_=row_part[:, 4 * lo : 4 * hi])
+            fo = tpsum.tile([P, 2 * NT], F32, tag="tp")
+            folded[lo] = fo
+            parts = [(row_sb[:, 4 * lo : 4 * hi], fo[:, lo:hi])]
+            if lo == 0:
+                parts.append((gram_part[:], fo[:, NT : NT + len(GRAM_TILES)]))
+            for src, dst in parts:
+                for s in range(4):
+                    nc.tensor.matmul(out=dst, lhsT=fold[:, s, :], rhs=src.rearrange("p (t s) -> p s t", s=4)[:, s, :], start=(s == 0), stop=(s == 3))
+
+        def norms(lo, hi):
+            fo = folded[lo]
+            cs = slice(lo, hi)
+            tt = nc.vector.tensor_tensor
+            tt(out=small["rows"][:, cs], in0=fo[:, cs], in1=small["rest"][:, cs], op=ALU.add)
+            tt(out=small["ss_a"][:, cs], in0=sq_sums[:, 2 * lo : 2 * hi : 2], in1=sq_sums[:, 2 * lo + 1 : 2 * hi : 2], op=ALU.add)
+            tt(out=small["rows2"][:, cs], in0=small["rows"][:, cs], in1=small["rows"][:, cs], op=ALU.mult)
+            tt(out=small["ss_b"][:, cs], in0=small["ss_a"][:, cs], in1=small["extra"][:, cs], op=ALU.add)
+            if lo == 0:
+                gt = slice(GRAM_TILES[0], NT, GRAM_STEP)
+                tt(out=small["ss_b"][:, gt], in0=fo[:, NT : NT + len(GRAM_TILES)], in1=small["extra"][:, gt], op=ALU.add)
+            tt(out=small["den"][:, cs], in0=small["rows2"][:, cs], in1=small["ss_b"][:, cs], op=ALU.subtract)
+            nc.vector.tensor_single_scalar(out=small["nz"][:, cs], in_=small["den"][:, cs], scalar=0.0, op=ALU.not_equal)
+            nc.vector.tensor_scalar(out=small["pad"][:, cs], in0=small["nz"][:, cs], scalar1=-1.0, scalar2=1.0, op0=ALU.mult, op1=ALU.add)
+            tt(out=small["safe"][:, cs], in0=small["den"][:, cs], in1=small["pad"][:, cs], op=ALU.add)
+            nc.vector.reciprocal(out=small["rec"][:, cs], in_=small["safe"][:, cs])
+            tt(out=small["norm"][:, cs], in0=small["rec"][:, cs], in1=small["nz"][:, cs], op=ALU.mult)
+
+        out_tiles = out.rearrange("(t p) c -> p t c", p=P)
+
+        def finish(lo, hi):
+            for t in range(lo, hi):
+                cols = slice(C * t, C * t + C)
+                nc.vector.scalar_tensor_tensor(
+                    out=result[:, cols], in0=result[:, cols], scalar=small["norm"][:, t : t + 1], in1=bias_bc[:], op0=ALU.mult, op1=ALU.add
+                )
+            nc.sync.dma_start(out=out_tiles[:, lo:hi, :], in_=result[:, C * lo : C * hi].rearrange("p (t c) -> p t c", c=C))
+
+        more_loads(0)
+        square_halves(H_FIRST)
+        for v in range(4):
+            build_mask(v)
+        build_fold()
+        transposes(0)
+        new_grouped(0)
+        diagonal_bank(0)
+        for h in bank_order(0)[1:]:
+            copy_bank(0, h, nc.vector.tensor_copy)
+        diagonal_adj(0)
+        diagonal_sq(0)
+        x_transposed()
+
+        in_stream = len(halves) - H_FIRST - H_TAIL
+        for i in range(NT):
+            nxt = i + 1
+            if i == 1:
+                xw_quantised()
+                diagonal_terms()
+            if nxt < NT:
+                transposes(nxt)
+            else:
+                row_sums(i)
+            if i >= 1:
+                mx(i - 1)
+                if i % 4 == 0:
+                    square_s(i // 4 - 1)
+            if nxt < NT:
+                row_sums(i)
+            if i in GRAM_TILES:
+                gram(i)
+            squares(i)
+            if nxt < NT:
+                new_grouped(nxt)
+                diagonal_bank(nxt)
+                for h in bank_order(nxt)[1:]:
+                    copy_bank(nxt, h, nc.scalar.copy)
+            if i == NT - 2:
+                fold_sums(0, ROUND_1)
+            if i == NT - 1:
+                fold_sums(ROUND_1, NT)
+            new_codes(i)
+            quantise(i, 0)
+            if nxt < NT:
+                diagonal_adj(nxt)
+            square_halves(H_FIRST + (in_stream * nxt) // NT)
+            if nxt < NT:
+                diagonal_sq(nxt)
+            quantise(i, 1)
+            if i in GRAM_TILES:
+                gram_diagonal(i)
+            if i >= 1 and i % 4 == 0:
+                minus_q(i // 4 - 1)
+            more_loads(nxt)
+
+        mx(NT - 1)
+        square_s(NT // 4 - 1)
+        square_halves(len(halves))
+        norms(0, ROUND_1)
+        for lo in range(0, ROUND_1, 8):
+            finish(lo, min(lo + 8, ROUND_1))
+        minus_q(NT // 4 - 1)
+        norms(ROUND_1, NT)
+        finish(ROUND_1, NT)

@@ -22,11 +22,10 @@ BANK = 512
 HALF = N // 2
 FLOPS = 2 * N * N * C * 2 + 2 * N * C * C
 
-GRAM_STEP = 8
-GRAM_TILES = (3, 11, 19, 27)
-E_BUFS = 6
-H_FIRST = 2
-H_TAIL = 2
+GRAM_STEP = 6
+GRAM_TILES = (2, 8, 14, 20, 26)
+E_BUFS = 7
+V_SLOTS = (3,)
 ROUND_1 = NT - 4
 
 
@@ -38,7 +37,9 @@ def tile_bgnna_kernel(tc, x, edge_index, weight, bias, out):
         gpool = ctx.enter_context(tc.tile_pool(name="gpool", bufs=3))
         cpool = ctx.enter_context(tc.tile_pool(name="cpool", bufs=3))
         work = ctx.enter_context(tc.tile_pool(name="work", bufs=2))
-        tpsum = ctx.enter_context(tc.psum_pool(name="tpsum", bufs=5))
+        spool = ctx.enter_context(tc.tile_pool(name="spool", bufs=3))
+        tpsum = ctx.enter_context(tc.psum_pool(name="tpsum", bufs=4))
+        opsum = ctx.enter_context(tc.psum_pool(name="opsum", bufs=2))
         apsum = ctx.enter_context(tc.psum_pool(name="apsum", bufs=1))
         ctx.enter_context(tc.manual_schedule())
 
@@ -60,16 +61,16 @@ def tile_bgnna_kernel(tc, x, edge_index, weight, bias, out):
         w_sb = const.tile([P, C], BF16)
         nc.sync.dma_start(out=w_sb[:], in_=weight)
         load(1, 1)
-        load(2, 1)
-        load(3, 1)
-        bias_bc = const.tile([P, C], BF16)
-        nc.sync.dma_start(out=bias_bc[:], in_=bias.partition_broadcast(P))
         diag_b = const.tile([P, NT], BF16)
         with nc.allow_non_contiguous_dma(reason="the 4096 diagonal elements, one each"):
             nc.sync.dma_start(
                 out=diag_b[:],
                 in_=edge_index.rearrange("a b -> (a b)")[0 : N * N : N + 1].rearrange("(t p) -> p t", p=P),
             )
+        load(2, 1)
+        load(3, 1)
+        bias_bc = const.tile([P, C], BF16)
+        nc.sync.dma_start(out=bias_bc[:], in_=bias.partition_broadcast(P))
 
         ident_f = const.tile([P, P], F32)
         make_identity(nc, ident_f[:])
@@ -77,17 +78,10 @@ def tile_bgnna_kernel(tc, x, edge_index, weight, bias, out):
         nc.gpsimd.memset(sq_sums[:], 0.0)
         fold = const.tile([P, 4, P], F32)
         nc.gpsimd.memset(fold[:], 0.0)
-        mask = const.tile([P, 4, PASS], BF16)
-        nc.vector.memset(mask[:], 0.0)
         ident_b = const.tile([P, P], BF16)
         nc.vector.tensor_copy(out=ident_b[:], in_=ident_f[:])
         ones_b = const.tile([P, 2], BF16)
         nc.vector.memset(ones_b[:], 1.0)
-
-        def build_mask(v):
-            view = mask[:, v, :].rearrange("p (h a t) -> p h a t", h=P // 4, a=4, t=4)
-            for a in range(4):
-                nc.vector.tensor_copy(out=view[:, :, a, a], in_=ident_b[:, 32 * v : 32 * v + 32])
 
         def build_fold():
             quarter = const.tile([P, 32], F32)
@@ -95,94 +89,109 @@ def tile_bgnna_kernel(tc, x, edge_index, weight, bias, out):
             for s in range(4):
                 nc.vector.tensor_copy(out=fold[:, s, 32 * s : 32 * s + 32], in_=quarter[:])
 
-        scrap = const.tile([P, N], BF16)
+        scrap = const.tile([P, HALF], BF16)
         result = const.tile([P, NT * C], F32)
         row_part = apsum.tile([P, 4 * NT], F32)
         gram_part = const.tile([P, 4 * len(GRAM_TILES)], F32)
         banks = {}
         grouped = {}
-        exact = {}
+        sq_nat = {}
+        sq_banks = {}
         codes = {}
         grams = {}
         products = {}
         squared = {}
 
-        halves = [(t, k) for t in range(NT) if t not in GRAM_TILES for k in range(2)]
-        progress = {"halves": 0, "loads": 4}
+        second = [t for t in range(NT) if t not in GRAM_TILES]
+        progress = {"second": 0, "loads": 4}
 
-        def square_halves(upto):
-            while progress["halves"] < upto:
-                t, k = halves[progress["halves"]]
-                cols = slice(HALF * k, HALF * k + HALF)
-                nc.scalar.activation(
-                    out=scrap[:, cols], in_=e_tiles[t][:, cols], func=ACT.Square, accum_out=sq_sums[:, 2 * t + k : 2 * t + k + 1]
-                )
-                progress["halves"] += 1
+        def d_half(t):
+            return t // 4 // (NG // 2)
 
-        def more_loads(transposed):
+        def square_half(t, half, out_ap):
+            cols = slice(HALF * half, HALF * half + HALF)
+            nc.scalar.activation(
+                out=out_ap, in_=e_tiles[t][:, cols], func=ACT.Square, accum_out=sq_sums[:, 2 * t + half : 2 * t + half + 1]
+            )
+
+        def square_first(t):
+            sq_n = spool.tile([P, HALF], BF16, name="sq_n")
+            sq_nat[t] = sq_n
+            if t in GRAM_TILES:
+                at = PASS * (t // 4 % (NG // 2))
+                e_d = e_tiles[t][:, PASS * (t // 4) : PASS * (t // 4) + PASS]
+                nc.vector.tensor_tensor(out=sq_n[:, at : at + PASS], in0=e_d, in1=e_d, op=ALU.mult)
+            else:
+                square_half(t, d_half(t), sq_n[:])
+
+        def square_second(upto):
+            while progress["second"] < upto:
+                t = second[progress["second"]]
+                square_half(t, 1 - d_half(t), scrap[:])
+                progress["second"] += 1
+
+        def more_loads(done):
             while progress["loads"] < NT:
                 old = progress["loads"] - E_BUFS
-                if old > transposed:
+                if old > done:
                     return
-                if old >= 0 and old not in GRAM_TILES and halves.index((old, 1)) >= progress["halves"]:
+                if old >= 0 and old not in GRAM_TILES and second.index(old) >= progress["second"]:
                     return
                 load(progress["loads"], 1)
                 progress["loads"] += 1
 
-        def bank_order(t):
-            first = (t // 4) // 2
-            return [first] + [h for h in range(4) if h != first]
+        def add_identity(t):
+            blk = e_tiles[t][:, P * t : P * t + P]
+            nc.vector.tensor_tensor(out=blk, in0=blk, in1=ident_b[:], op=ALU.add)
+
+        def mend_sq(t):
+            at = PASS * (t // 4 % (NG // 2)) + P * (t % 4)
+            blk = sq_nat[t][:, at : at + P]
+            nc.vector.scalar_tensor_tensor(
+                out=blk, in0=ident_b[:], scalar=small["mend"][:, t : t + 1], in1=blk, op0=ALU.mult, op1=ALU.add
+            )
+
+        def passes(t):
+            return [t // 4] + [g for g in range(NG) if g != t // 4]
+
+        def transpose_pass(out_ap, words, w0):
+            for u in range(2):
+                nc.tensor.transpose(out=out_ap[:, P * u : P * u + P], in_=words[:, w0 + u : w0 + 256 : 2], identity=ident_f[:])
 
         def transposes(t):
             words = e_tiles[t][:].bitcast(F32)
-            for h in bank_order(t):
+            order = passes(t)
+            for b in range(4):
                 tp = tpsum.tile([P, BANK], F32, tag="tp")
-                banks[(t, h)] = tp
-                for k in range(4):
-                    g, u = 2 * h + k // 2, k % 2
-                    nc.tensor.transpose(out=tp[:, P * k : P * k + P], in_=words[:, 256 * g + u : 256 * (g + 1) : 2], identity=ident_f[:])
+                banks[(t, b)] = tp
+                for j in range(2):
+                    transpose_pass(tp[:, 256 * j : 256 * j + 256], words, 256 * order[2 * b + j])
+
+        def sq_transposes(t):
+            tp = opsum.tile([P, BANK], F32, tag="op")
+            sq_banks[t] = tp
+            transpose_pass(tp[:, 0:256], sq_nat[t][:].bitcast(F32), 256 * (t // 4 % (NG // 2)))
 
         def new_grouped(t):
             adj_g = gpool.tile([P, N], BF16, name="adj_g", align_bytes=64)
             sq_g = gpool.tile([P, N], BF16, name="sq_g", align_bytes=64)
             grouped[t] = (adj_g, sq_g)
 
-        def copy_bank(t, h, engine_copy):
+        def group_bank(t, b, engine_copy):
             engine_copy(
-                out=grouped[t][0][:].bitcast(F32)[:, BANK * h : BANK * h + BANK].rearrange("p (g i u) -> p g i u", g=2, i=P, u=2),
-                in_=banks[(t, h)][:].rearrange("p (g u i) -> p g i u", g=2, u=2, i=P),
+                out=grouped[t][0][:].bitcast(F32)[:, BANK * b : BANK * b + BANK].rearrange("p (g i u) -> p g i u", g=2, i=P, u=2),
+                in_=banks[(t, b)][:].rearrange("p (g u i) -> p g i u", g=2, u=2, i=P),
             )
 
-        def diagonal_bank(t):
-            g_d = t // 4
-            tp = banks[(t, g_d // 2)]
-            at = 256 * (g_d % 2)
-            other = 256 - at
-            adj_x = work.tile([P, PASS], F32, name="adj_x")
-            exact[t] = adj_x
-            nc.vector.tensor_tensor(
-                out=adj_x[:].rearrange("p (i u e) -> p i u e", i=P, u=2, e=2),
-                in0=tp[:].bitcast(BF16)[:, 2 * at : 2 * at + PASS].rearrange("p (u i e) -> p i u e", u=2, i=P, e=2),
-                in1=mask[:, t % 4, :].rearrange("p (i u e) -> p i u e", i=P, u=2, e=2),
-                op=ALU.add,
+        def group_sq(t, engine_copy):
+            engine_copy(
+                out=grouped[t][1][:].bitcast(F32)[:, 0:256].rearrange("p (i u) -> p i u", i=P, u=2),
+                in_=sq_banks[t][:, 0:256].rearrange("p (u i) -> p i u", u=2, i=P),
             )
-            w0 = BANK * (g_d // 2) + other
-            nc.vector.tensor_copy(
-                out=grouped[t][0][:].bitcast(F32)[:, w0 : w0 + 256].rearrange("p (i u) -> p i u", i=P, u=2),
-                in_=tp[:, other : other + 256].rearrange("p (u i) -> p i u", u=2, i=P),
-            )
-
-        def diagonal_adj(t):
-            nc.vector.tensor_copy(out=grouped[t][0][:, PASS * (t // 4) : PASS * (t // 4) + PASS], in_=exact[t][:])
-
-        def diagonal_sq(t):
-            nc.scalar.activation(out=grouped[t][1][:, PASS * (t // 4) : PASS * (t // 4) + PASS], in_=exact[t][:], func=ACT.Square)
 
         def squares(t):
             adj_g, sq_g = grouped[t]
-            for lo, hi in ((0, PASS * (t // 4)), (PASS * (t // 4) + PASS, N)):
-                if hi > lo:
-                    nc.vector.tensor_tensor(out=sq_g[:, lo:hi], in0=adj_g[:, lo:hi], in1=adj_g[:, lo:hi], op=ALU.mult)
+            nc.vector.tensor_tensor(out=sq_g[:, PASS:N], in0=adj_g[:, PASS:N], in1=adj_g[:, PASS:N], op=ALU.mult)
 
         def new_codes(t):
             a_c = cpool.tile([P, N // 4], U32, name="a_c", align_bytes=64)
@@ -206,7 +215,7 @@ def tile_bgnna_kernel(tc, x, edge_index, weight, bias, out):
 
         def gram(t):
             adj_g = grouped[t][0]
-            gr = tpsum.tile([P, BANK], F32, tag="tp")
+            gr = opsum.tile([P, BANK], F32, tag="op")
             grams[t] = gr
             for s in range(4):
                 for g in range(NG):
@@ -229,32 +238,40 @@ def tile_bgnna_kernel(tc, x, edge_index, weight, bias, out):
         xw_codes = []
 
         def mx(t):
-            if t % 4 == 0:
-                s_ps = apsum.tile([P, BANK], F32, name="s_ps")
-                q_ps = apsum.tile([P, BANK], F32, name="q_ps")
-                products[t // 4] = (s_ps, q_ps)
+            if t == NT - 1:
+                sq_ps = opsum.tile([P, 2, 2, P], F32, tag="op")
+                products[t] = sq_ps
+            elif t % 2 == 0:
+                sq_ps = apsum.tile([P, 2, 2, P], F32, name="sq_ps")
+                products[t] = products[t + 1] = sq_ps
             for which in range(2):
                 l_c, l_s = codes[t][which]
                 r_c, r_s = xw_codes[which]
-                for g in range(NG):
-                    cols = slice(P * g, P * g + P)
+                for slot, g in enumerate(passes(t)):
+                    lc = slice(P * slot, P * slot + P)
+                    rc = slice(P * g, P * g + P)
                     nc.tensor.matmul_mx(
-                        out=products[t // 4][which][:, P * (t % 4) : P * (t % 4) + P],
-                        lhsT=l_c[:, cols].bitcast(FP8X4),
-                        lhsT_scale=l_s[:, cols],
-                        rhs=r_c[:, cols].bitcast(FP8X4),
-                        rhs_scale=r_s[:, cols],
-                        start=(g == 0),
-                        stop=(g == NG - 1),
+                        out=products[t][:, which, t % 2, :],
+                        lhsT=l_c[:, lc].bitcast(FP8X4),
+                        lhsT_scale=l_s[:, lc],
+                        rhs=r_c[:, rc].bitcast(FP8X4),
+                        rhs_scale=r_s[:, rc],
+                        start=(slot == 0),
+                        stop=(slot == NG - 1),
                     )
 
-        def square_s(b):
-            s2 = work.tile([P, BANK], F32, name="s2")
-            squared[b] = s2
-            nc.scalar.activation(out=s2[:], in_=products[b][0][:], func=ACT.Square)
+        def square_s(lo, hi):
+            s2 = work.tile([P, 2, P], F32, name="s2")
+            squared[lo] = s2
+            nc.scalar.activation(out=s2[:, 0 : hi - lo, :], in_=products[lo][:, 0, lo % 2 : lo % 2 + hi - lo, :], func=ACT.Square)
 
-        def minus_q(b):
-            nc.vector.tensor_tensor(out=result[:, BANK * b : BANK * b + BANK], in0=squared[b][:], in1=products[b][1][:], op=ALU.subtract)
+        def minus_q(lo, hi):
+            nc.vector.tensor_tensor(
+                out=result[:, C * lo : C * hi].rearrange("p (t c) -> p t c", c=C),
+                in0=squared[lo][:, 0 : hi - lo, :],
+                in1=products[lo][:, 1, lo % 2 : lo % 2 + hi - lo, :],
+                op=ALU.subtract,
+            )
 
         xt_sb = const.tile([P, N], BF16)
         xw_g = const.tile([P, N], BF16, align_bytes=64)
@@ -266,9 +283,9 @@ def tile_bgnna_kernel(tc, x, edge_index, weight, bias, out):
                 for j in range(8):
                     b = 8 * k + j
                     nc.tensor.transpose(out=xtp[:, P * j : P * j + P], in_=x_sb[:, P * b : P * b + P], identity=ident_b[:])
-                nc.scalar.copy(out=xt_sb[:, 1024 * k : 1024 * k + 1024], in_=xtp[:])
+                (nc.vector.tensor_copy if k % 2 == 0 else nc.scalar.copy)(out=xt_sb[:, 1024 * k : 1024 * k + 1024], in_=xtp[:])
 
-        def xw_quantised():
+        def xw_grouped():
             for g in range(NG):
                 xwp = tpsum.tile([P, BANK], F32, tag="tp")
                 for t in range(4):
@@ -279,34 +296,38 @@ def tile_bgnna_kernel(tc, x, edge_index, weight, bias, out):
                 nc.scalar.activation(
                     out=xw2_g[:, cols].rearrange("p (c t) -> p c t", t=4), in_=xwp[:].rearrange("p (t c) -> p c t", t=4), func=ACT.Square
                 )
-            for name, src in (("xw", xw_g), ("xw2", xw2_g)):
-                words = const.tile([P, N // 4], U32, name=name + "_c", align_bytes=64)
-                scales = const.tile([P, N // 4], U8, name=name + "_s", align_bytes=64)
-                xw_codes.append((words, scales))
-                nc.vector.quantize_mx(out=words[:].bitcast(FP8X4), scales=scales[:], in_=src[:])
+
+        def xw_quantised(which):
+            words = const.tile([P, N // 4], U32, name=("xw_c", "xw2_c")[which], align_bytes=64)
+            scales = const.tile([P, N // 4], U8, name=("xw_s", "xw2_s")[which], align_bytes=64)
+            xw_codes.append((words, scales))
+            nc.vector.quantize_mx(out=words[:].bitcast(FP8X4), scales=scales[:], in_=(xw_g, xw2_g)[which][:])
 
         small = {}
-        for name in ("diag", "one_d", "rest", "extra", "sq_x", "sq_r", "rows", "rows2", "ss_a", "ss_b", "ss_c", "den", "nz", "pad", "safe", "rec", "norm"):
+        for name in ("diag", "one_d", "rest", "extra", "sq_x", "sq_r", "mend", "rows", "rows2", "ss_a", "ss_b", "ss_c", "den", "zero", "safe", "keep", "rec", "norm"):
             small[name] = const.tile([P, NT], F32, name=name)
         one_d_b = const.tile([P, NT], BF16)
+        sq_x_b = const.tile([P, NT], BF16)
+        sq_r_b = const.tile([P, NT], BF16)
 
         def diagonal_terms():
-            gt = slice(GRAM_TILES[0], NT, GRAM_STEP)
             nc.vector.tensor_copy(out=small["diag"][:], in_=diag_b[:])
             nc.vector.tensor_scalar_add(out=small["one_d"][:], in0=small["diag"][:], scalar1=1.0)
             nc.vector.tensor_copy(out=one_d_b[:], in_=small["one_d"][:])
-            nc.vector.tensor_tensor(out=small["rest"][:], in0=small["one_d"][:], in1=one_d_b[:], op=ALU.subtract)
-            nc.vector.tensor_scalar(out=small["extra"][:], in0=small["diag"][:], scalar1=2.0, scalar2=1.0, op0=ALU.mult, op1=ALU.add)
             nc.vector.tensor_tensor(out=small["sq_x"][:], in0=small["one_d"][:], in1=small["one_d"][:], op=ALU.mult)
             nc.vector.tensor_tensor(out=small["sq_r"][:], in0=one_d_b[:], in1=one_d_b[:], op=ALU.mult)
-            nc.vector.tensor_tensor(out=small["extra"][:, gt], in0=small["sq_x"][:, gt], in1=small["sq_r"][:, gt], op=ALU.subtract)
+            nc.vector.tensor_copy(out=sq_x_b[:], in_=small["sq_x"][:])
+            nc.vector.tensor_copy(out=sq_r_b[:], in_=small["sq_r"][:])
+            nc.vector.tensor_tensor(out=small["mend"][:], in0=sq_x_b[:], in1=sq_r_b[:], op=ALU.subtract)
+            nc.vector.tensor_tensor(out=small["rest"][:], in0=small["one_d"][:], in1=one_d_b[:], op=ALU.subtract)
+            nc.vector.tensor_tensor(out=small["extra"][:], in0=small["sq_x"][:], in1=small["sq_r"][:], op=ALU.subtract)
 
         row_sb = const.tile([P, 4 * NT], F32)
         folded = {}
 
         def fold_sums(lo, hi):
             nc.vector.tensor_copy(out=row_sb[:, 4 * lo : 4 * hi], in_=row_part[:, 4 * lo : 4 * hi])
-            fo = tpsum.tile([P, 2 * NT], F32, tag="tp")
+            fo = opsum.tile([P, 2 * NT], F32, tag="op")
             folded[lo] = fo
             parts = [(row_sb[:, 4 * lo : 4 * hi], fo[:, lo:hi])]
             if lo == 0:
@@ -315,23 +336,27 @@ def tile_bgnna_kernel(tc, x, edge_index, weight, bias, out):
                 for s in range(4):
                     nc.tensor.matmul(out=dst, lhsT=fold[:, s, :], rhs=src.rearrange("p (t s) -> p s t", s=4)[:, s, :], start=(s == 0), stop=(s == 3))
 
-        def norms(lo, hi):
+        def norms_v(lo, hi):
             fo = folded[lo]
             cs = slice(lo, hi)
-            tt = nc.vector.tensor_tensor
-            tt(out=small["rows"][:, cs], in0=fo[:, cs], in1=small["rest"][:, cs], op=ALU.add)
-            tt(out=small["ss_a"][:, cs], in0=sq_sums[:, 2 * lo : 2 * hi : 2], in1=sq_sums[:, 2 * lo + 1 : 2 * hi : 2], op=ALU.add)
-            tt(out=small["rows2"][:, cs], in0=small["rows"][:, cs], in1=small["rows"][:, cs], op=ALU.mult)
-            tt(out=small["ss_b"][:, cs], in0=small["ss_a"][:, cs], in1=small["extra"][:, cs], op=ALU.add)
+            sm = {name: tile[:, cs] for name, tile in small.items()}
+            gp = nc.gpsimd
+            nc.vector.tensor_tensor(out=sm["rows"], in0=fo[:, cs], in1=sm["rest"], op=ALU.add)
             if lo == 0:
-                gt = slice(GRAM_TILES[0], NT, GRAM_STEP)
-                tt(out=small["ss_b"][:, gt], in0=fo[:, NT : NT + len(GRAM_TILES)], in1=small["extra"][:, gt], op=ALU.add)
-            tt(out=small["den"][:, cs], in0=small["rows2"][:, cs], in1=small["ss_b"][:, cs], op=ALU.subtract)
-            nc.vector.tensor_single_scalar(out=small["nz"][:, cs], in_=small["den"][:, cs], scalar=0.0, op=ALU.not_equal)
-            nc.vector.tensor_scalar(out=small["pad"][:, cs], in0=small["nz"][:, cs], scalar1=-1.0, scalar2=1.0, op0=ALU.mult, op1=ALU.add)
-            tt(out=small["safe"][:, cs], in0=small["den"][:, cs], in1=small["pad"][:, cs], op=ALU.add)
-            nc.vector.reciprocal(out=small["rec"][:, cs], in_=small["safe"][:, cs])
-            tt(out=small["norm"][:, cs], in0=small["rec"][:, cs], in1=small["nz"][:, cs], op=ALU.mult)
+                gt = slice(2 * GRAM_TILES[0], 2 * hi, 2 * GRAM_STEP)
+                nc.vector.tensor_copy(out=sq_sums[:, gt], in_=fo[:, NT : NT + len(GRAM_TILES)])
+            gp.tensor_tensor(out=sm["rows2"], in0=sm["rows"], in1=sm["rows"], op=ALU.mult)
+            gp.tensor_tensor(out=sm["ss_a"], in0=sq_sums[:, 2 * lo : 2 * hi : 2], in1=sq_sums[:, 2 * lo + 1 : 2 * hi : 2], op=ALU.add)
+            gp.tensor_tensor(out=sm["ss_b"], in0=sm["ss_a"], in1=sm["extra"], op=ALU.add)
+            gp.tensor_tensor(out=sm["den"], in0=sm["rows2"], in1=sm["ss_b"], op=ALU.subtract)
+            gp.tensor_scalar(out=sm["zero"], in0=sm["den"], scalar1=0.0, scalar2=1.0, op0=ALU.is_equal, op1=ALU.mult)
+            gp.tensor_tensor(out=sm["safe"], in0=sm["den"], in1=sm["zero"], op=ALU.add)
+            gp.tensor_scalar(out=sm["keep"], in0=sm["zero"], scalar1=-1.0, scalar2=1.0, op0=ALU.mult, op1=ALU.add)
+
+        def norms_rec(lo, hi):
+            sm = {name: tile[:, lo:hi] for name, tile in small.items()}
+            nc.vector.reciprocal(out=sm["rec"], in_=sm["safe"])
+            nc.gpsimd.tensor_tensor(out=sm["norm"], in0=sm["rec"], in1=sm["keep"], op=ALU.mult)
 
         out_tiles = out.rearrange("(t p) c -> p t c", p=P)
 
@@ -344,67 +369,97 @@ def tile_bgnna_kernel(tc, x, edge_index, weight, bias, out):
             nc.sync.dma_start(out=out_tiles[:, lo:hi, :], in_=result[:, C * lo : C * hi].rearrange("p (t c) -> p t c", c=C))
 
         more_loads(0)
-        square_halves(H_FIRST)
-        for v in range(4):
-            build_mask(v)
+        add_identity(0)
         build_fold()
         transposes(0)
         new_grouped(0)
-        diagonal_bank(0)
-        for h in bank_order(0)[1:]:
-            copy_bank(0, h, nc.vector.tensor_copy)
-        diagonal_adj(0)
-        diagonal_sq(0)
+        for b in range(4):
+            group_bank(0, b, nc.vector.tensor_copy if b % 2 == 0 else nc.scalar.copy)
+        square_first(0)
+        squares(0)
+        row_sums(0)
         x_transposed()
+        new_codes(0)
+        quantise(0, 0)
+        xw_grouped()
+        add_identity(1)
+        transposes(1)
+        new_grouped(1)
+        for b in range(4):
+            group_bank(1, b, nc.vector.tensor_copy if b in V_SLOTS else nc.scalar.copy)
+        diagonal_terms()
+        mend_sq(0)
+        sq_transposes(0)
+        add_identity(2)
+        transposes(2)
+        group_sq(0, nc.scalar.copy)
+        square_first(1)
+        xw_quantised(0)
+        quantise(0, 1)
+        xw_quantised(1)
+        mend_sq(1)
+        sq_transposes(1)
+        add_identity(3)
+        add_identity(4)
+        group_sq(1, nc.scalar.copy)
+        square_first(2)
+        square_second(1)
+        more_loads(2)
 
-        in_stream = len(halves) - H_FIRST - H_TAIL
-        for i in range(NT):
+        for i in range(1, NT):
             nxt = i + 1
-            if i == 1:
-                xw_quantised()
-                diagonal_terms()
-            if nxt < NT:
-                transposes(nxt)
-            else:
+            if i == NT - 1:
                 row_sums(i)
-            if i >= 1:
-                mx(i - 1)
-                if i % 4 == 0:
-                    square_s(i // 4 - 1)
+            mx(i - 1)
+            squares(i)
             if nxt < NT:
                 row_sums(i)
             if i in GRAM_TILES:
                 gram(i)
-            squares(i)
             if nxt < NT:
                 new_grouped(nxt)
-                diagonal_bank(nxt)
-                for h in bank_order(nxt)[1:]:
-                    copy_bank(nxt, h, nc.scalar.copy)
-            if i == NT - 2:
-                fold_sums(0, ROUND_1)
+                for b in range(4):
+                    group_bank(nxt, b, nc.vector.tensor_copy if b in V_SLOTS else nc.scalar.copy)
+                mend_sq(nxt)
+                sq_transposes(nxt)
+            if i % 2 == 0:
+                square_s(i - 2, i)
+            if i + 2 < NT:
+                transposes(i + 2)
+                square_first(i + 2)
             if i == NT - 1:
+                square_s(NT - 2, NT - 1)
                 fold_sums(ROUND_1, NT)
             new_codes(i)
             quantise(i, 0)
+            if i + 4 < NT:
+                add_identity(i + 4)
+            square_second(len(second) if i >= NT - 2 else (len(second) * nxt) // NT)
             if nxt < NT:
-                diagonal_adj(nxt)
-            square_halves(H_FIRST + (in_stream * nxt) // NT)
-            if nxt < NT:
-                diagonal_sq(nxt)
+                group_sq(nxt, nc.scalar.copy)
+            if i == NT - 3:
+                fold_sums(0, ROUND_1)
+            if i == NT - 2:
+                norms_v(0, ROUND_1)
+            if i == NT - 1:
+                norms_v(ROUND_1, NT)
             quantise(i, 1)
+            if i == NT - 2:
+                norms_rec(0, ROUND_1)
             if i in GRAM_TILES:
                 gram_diagonal(i)
-            if i >= 1 and i % 4 == 0:
-                minus_q(i // 4 - 1)
-            more_loads(nxt)
+            if i % 2 == 0:
+                minus_q(i - 2, i)
+            more_loads(i + 2)
 
         mx(NT - 1)
-        square_s(NT // 4 - 1)
-        square_halves(len(halves))
-        norms(0, ROUND_1)
-        for lo in range(0, ROUND_1, 8):
-            finish(lo, min(lo + 8, ROUND_1))
-        minus_q(NT // 4 - 1)
-        norms(ROUND_1, NT)
-        finish(ROUND_1, NT)
+        square_s(NT - 1, NT)
+        finish(0, 8)
+        finish(8, 16)
+        finish(16, 24)
+        norms_rec(ROUND_1, NT)
+        finish(24, ROUND_1)
+        minus_q(NT - 2, NT - 1)
+        finish(ROUND_1, NT - 1)
+        minus_q(NT - 1, NT)
+        finish(NT - 1, NT)

@@ -22,11 +22,11 @@ BANK = 512
 HALF = N // 2
 FLOPS = 2 * N * N * C * 2 + 2 * N * C * C
 
-GRAM_STEP = 6
-GRAM_TILES = (2, 8, 14, 20, 26)
+GRAM_STEP = 5
+GRAM_TILES = (2, 7, 12, 17, 22)
 E_BUFS = 7
 V_SLOTS = (3,)
-ROUND_1 = NT - 4
+ROUND_1 = NT - 8
 
 
 def tile_bgnna_kernel(tc, x, edge_index, weight, bias, out):
@@ -158,10 +158,10 @@ def tile_bgnna_kernel(tc, x, edge_index, weight, bias, out):
             for u in range(2):
                 nc.tensor.transpose(out=out_ap[:, P * u : P * u + P], in_=words[:, w0 + u : w0 + 256 : 2], identity=ident_f[:])
 
-        def transposes(t):
+        def transposes(t, which_banks=(0, 1, 2, 3)):
             words = e_tiles[t][:].bitcast(F32)
             order = passes(t)
-            for b in range(4):
+            for b in which_banks:
                 tp = tpsum.tile([P, BANK], F32, tag="tp")
                 banks[(t, b)] = tp
                 for j in range(2):
@@ -213,11 +213,13 @@ def tile_bgnna_kernel(tc, x, edge_index, weight, bias, out):
                         out=row_part[:, 4 * t + s : 4 * t + s + 1], lhsT=adj_g[:, c0 : c0 + P], rhs=ones_b[:, 0:1], start=(g == 0), stop=(g == NG - 1)
                     )
 
-        def gram(t):
+        def gram(t, groups):
             adj_g = grouped[t][0]
-            gr = opsum.tile([P, BANK], F32, tag="op")
-            grams[t] = gr
-            for s in range(4):
+            if t not in grams:
+                gr = opsum.tile([P, BANK], F32, tag="op")
+                grams[t] = gr
+            gr = grams[t]
+            for s in groups:
                 for g in range(NG):
                     c0 = PASS * g + P * s
                     nc.tensor.matmul(
@@ -237,28 +239,27 @@ def tile_bgnna_kernel(tc, x, edge_index, weight, bias, out):
 
         xw_codes = []
 
-        def mx(t):
-            if t == NT - 1:
+        def mx(t, which):
+            if t == NT - 1 and t not in products:
                 sq_ps = opsum.tile([P, 2, 2, P], F32, tag="op")
                 products[t] = sq_ps
-            elif t % 2 == 0:
+            elif t not in products:
                 sq_ps = apsum.tile([P, 2, 2, P], F32, name="sq_ps")
                 products[t] = products[t + 1] = sq_ps
-            for which in range(2):
-                l_c, l_s = codes[t][which]
-                r_c, r_s = xw_codes[which]
-                for slot, g in enumerate(passes(t)):
-                    lc = slice(P * slot, P * slot + P)
-                    rc = slice(P * g, P * g + P)
-                    nc.tensor.matmul_mx(
-                        out=products[t][:, which, t % 2, :],
-                        lhsT=l_c[:, lc].bitcast(FP8X4),
-                        lhsT_scale=l_s[:, lc],
-                        rhs=r_c[:, rc].bitcast(FP8X4),
-                        rhs_scale=r_s[:, rc],
-                        start=(slot == 0),
-                        stop=(slot == NG - 1),
-                    )
+            l_c, l_s = codes[t][which]
+            r_c, r_s = xw_codes[which]
+            for slot, g in enumerate(passes(t)):
+                lc = slice(P * slot, P * slot + P)
+                rc = slice(P * g, P * g + P)
+                nc.tensor.matmul_mx(
+                    out=products[t][:, which, t % 2, :],
+                    lhsT=l_c[:, lc].bitcast(FP8X4),
+                    lhsT_scale=l_s[:, lc],
+                    rhs=r_c[:, rc].bitcast(FP8X4),
+                    rhs_scale=r_s[:, rc],
+                    start=(slot == 0),
+                    stop=(slot == NG - 1),
+                )
 
         def square_s(lo, hi):
             s2 = work.tile([P, 2, P], F32, name="s2")
@@ -304,7 +305,7 @@ def tile_bgnna_kernel(tc, x, edge_index, weight, bias, out):
             nc.vector.quantize_mx(out=words[:].bitcast(FP8X4), scales=scales[:], in_=(xw_g, xw2_g)[which][:])
 
         small = {}
-        for name in ("diag", "one_d", "rest", "extra", "sq_x", "sq_r", "mend", "rows", "rows2", "ss_a", "ss_b", "ss_c", "den", "zero", "safe", "keep", "rec", "norm"):
+        for name in ("diag", "one_d", "rest", "extra", "sq_x", "sq_r", "mend", "rows", "rows2", "ss_a", "ss_b", "den", "safe", "rec", "norm"):
             small[name] = const.tile([P, NT], F32, name=name)
         one_d_b = const.tile([P, NT], BF16)
         sq_x_b = const.tile([P, NT], BF16)
@@ -336,36 +337,36 @@ def tile_bgnna_kernel(tc, x, edge_index, weight, bias, out):
                 for s in range(4):
                     nc.tensor.matmul(out=dst, lhsT=fold[:, s, :], rhs=src.rearrange("p (t s) -> p s t", s=4)[:, s, :], start=(s == 0), stop=(s == 3))
 
-        def norms_v(lo, hi):
-            fo = folded[lo]
-            cs = slice(lo, hi)
-            sm = {name: tile[:, cs] for name, tile in small.items()}
-            gp = nc.gpsimd
-            nc.vector.tensor_tensor(out=sm["rows"], in0=fo[:, cs], in1=sm["rest"], op=ALU.add)
-            if lo == 0:
-                gt = slice(2 * GRAM_TILES[0], 2 * hi, 2 * GRAM_STEP)
-                nc.vector.tensor_copy(out=sq_sums[:, gt], in_=fo[:, NT : NT + len(GRAM_TILES)])
-            gp.tensor_tensor(out=sm["rows2"], in0=sm["rows"], in1=sm["rows"], op=ALU.mult)
-            gp.tensor_tensor(out=sm["ss_a"], in0=sq_sums[:, 2 * lo : 2 * hi : 2], in1=sq_sums[:, 2 * lo + 1 : 2 * hi : 2], op=ALU.add)
-            gp.tensor_tensor(out=sm["ss_b"], in0=sm["ss_a"], in1=sm["extra"], op=ALU.add)
-            gp.tensor_tensor(out=sm["den"], in0=sm["rows2"], in1=sm["ss_b"], op=ALU.subtract)
-            gp.tensor_scalar(out=sm["zero"], in0=sm["den"], scalar1=0.0, scalar2=1.0, op0=ALU.is_equal, op1=ALU.mult)
-            gp.tensor_tensor(out=sm["safe"], in0=sm["den"], in1=sm["zero"], op=ALU.add)
-            gp.tensor_scalar(out=sm["keep"], in0=sm["zero"], scalar1=-1.0, scalar2=1.0, op0=ALU.mult, op1=ALU.add)
-
-        def norms_rec(lo, hi):
+        def norm_steps(lo, hi):
             sm = {name: tile[:, lo:hi] for name, tile in small.items()}
-            nc.vector.reciprocal(out=sm["rec"], in_=sm["safe"])
-            nc.gpsimd.tensor_tensor(out=sm["norm"], in0=sm["rec"], in1=sm["keep"], op=ALU.mult)
+            tt = nc.vector.tensor_tensor
+            stt = nc.vector.scalar_tensor_tensor
+
+            def gram_sums():
+                gt = slice(2 * GRAM_TILES[0], 2 * hi, 2 * GRAM_STEP)
+                nc.vector.tensor_copy(out=sq_sums[:, gt], in_=folded[lo][:, NT : NT + len(GRAM_TILES)])
+
+            sums = [
+                lambda: tt(out=sm["rows"], in0=folded[lo][:, lo:hi], in1=sm["rest"], op=ALU.add),
+                lambda: tt(out=sm["ss_a"], in0=sq_sums[:, 2 * lo : 2 * hi : 2], in1=sq_sums[:, 2 * lo + 1 : 2 * hi : 2], op=ALU.add),
+                lambda: tt(out=sm["rows2"], in0=sm["rows"], in1=sm["rows"], op=ALU.mult),
+                lambda: tt(out=sm["ss_b"], in0=sm["ss_a"], in1=sm["extra"], op=ALU.add),
+                lambda: tt(out=sm["den"], in0=sm["rows2"], in1=sm["ss_b"], op=ALU.subtract),
+                lambda: stt(out=sm["safe"], in0=sm["den"], scalar=0.0, in1=sm["den"], op0=ALU.is_equal, op1=ALU.add),
+                lambda: nc.vector.reciprocal(out=sm["rec"], in_=sm["safe"]),
+                lambda: stt(out=sm["norm"], in0=sm["den"], scalar=0.0, in1=sm["rec"], op0=ALU.not_equal, op1=ALU.mult),
+            ]
+            return ([gram_sums] if lo == 0 else []) + sums
 
         out_tiles = out.rearrange("(t p) c -> p t c", p=P)
 
-        def finish(lo, hi):
-            for t in range(lo, hi):
-                cols = slice(C * t, C * t + C)
-                nc.vector.scalar_tensor_tensor(
-                    out=result[:, cols], in0=result[:, cols], scalar=small["norm"][:, t : t + 1], in1=bias_bc[:], op0=ALU.mult, op1=ALU.add
-                )
+        def finish(t):
+            cols = slice(C * t, C * t + C)
+            nc.vector.scalar_tensor_tensor(
+                out=result[:, cols], in0=result[:, cols], scalar=small["norm"][:, t : t + 1], in1=bias_bc[:], op0=ALU.mult, op1=ALU.add
+            )
+
+        def store(lo, hi):
             nc.sync.dma_start(out=out_tiles[:, lo:hi, :], in_=result[:, C * lo : C * hi].rearrange("p (t c) -> p t c", c=C))
 
         more_loads(0)
@@ -401,65 +402,73 @@ def tile_bgnna_kernel(tc, x, edge_index, weight, bias, out):
         sq_transposes(1)
         add_identity(3)
         add_identity(4)
-        group_sq(1, nc.scalar.copy)
         square_first(2)
         square_second(1)
         more_loads(2)
 
         for i in range(1, NT):
             nxt = i + 1
+            steps = norm_steps(0, ROUND_1) if i == ROUND_1 + 3 else norm_steps(ROUND_1, NT) if i == NT - 1 else []
             if i == NT - 1:
                 row_sums(i)
-            mx(i - 1)
+                fold_sums(ROUND_1, NT)
+            mx(i - 1, 0)
+            mx(i - 1, 1)
             squares(i)
+            for step in steps[0:2]:
+                step()
             if nxt < NT:
                 row_sums(i)
-            if i in GRAM_TILES:
-                gram(i)
-            if nxt < NT:
                 new_grouped(nxt)
                 for b in range(4):
-                    group_bank(nxt, b, nc.vector.tensor_copy if b in V_SLOTS else nc.scalar.copy)
+                    group_bank(nxt, b, nc.vector.tensor_copy if b == 3 or (b == 2 and nxt % 4 == 0) else nc.scalar.copy)
                 mend_sq(nxt)
-                sq_transposes(nxt)
+            group_sq(i, nc.scalar.copy)
+            for step in steps[2:4]:
+                step()
             if i % 2 == 0:
                 square_s(i - 2, i)
             if i + 2 < NT:
                 transposes(i + 2)
                 square_first(i + 2)
+            if nxt < NT:
+                sq_transposes(nxt)
+            if i in GRAM_TILES:
+                gram(i, range(4))
             if i == NT - 1:
                 square_s(NT - 2, NT - 1)
-                fold_sums(ROUND_1, NT)
+            if i == ROUND_1 + 2:
+                fold_sums(0, ROUND_1)
             new_codes(i)
             quantise(i, 0)
+            if i - 1 in GRAM_TILES:
+                gram_diagonal(i - 1)
+            for step in steps[4:6]:
+                step()
             if i + 4 < NT:
                 add_identity(i + 4)
             square_second(len(second) if i >= NT - 2 else (len(second) * nxt) // NT)
-            if nxt < NT:
-                group_sq(nxt, nc.scalar.copy)
-            if i == NT - 3:
-                fold_sums(0, ROUND_1)
-            if i == NT - 2:
-                norms_v(0, ROUND_1)
-            if i == NT - 1:
-                norms_v(ROUND_1, NT)
+            if i > ROUND_1 + 3:
+                for t in range(6 * (i - ROUND_1 - 4), 6 * (i - ROUND_1 - 3)):
+                    finish(t)
+                if i % 2 == 1:
+                    store(6 * (i - ROUND_1 - 5), 6 * (i - ROUND_1 - 3))
             quantise(i, 1)
-            if i == NT - 2:
-                norms_rec(0, ROUND_1)
-            if i in GRAM_TILES:
-                gram_diagonal(i)
+            for step in steps[6:7]:
+                step()
             if i % 2 == 0:
                 minus_q(i - 2, i)
+            for step in steps[7:]:
+                step()
             more_loads(i + 2)
 
-        mx(NT - 1)
+        mx(NT - 1, 0)
+        mx(NT - 1, 1)
         square_s(NT - 1, NT)
-        finish(0, 8)
-        finish(8, 16)
-        finish(16, 24)
-        norms_rec(ROUND_1, NT)
-        finish(24, ROUND_1)
         minus_q(NT - 2, NT - 1)
-        finish(ROUND_1, NT - 1)
+        for t in range(ROUND_1, NT - 1):
+            finish(t)
+        store(ROUND_1, NT - 1)
         minus_q(NT - 1, NT)
-        finish(NT - 1, NT)
+        finish(NT - 1)
+        store(NT - 1, NT)

@@ -421,7 +421,7 @@ def tile_bgnna_kernel(tc, x, edge_index, weight, bias, out):
                 row_sums(i)
                 new_grouped(nxt)
                 for b in range(4):
-                    group_bank(nxt, b, nc.vector.tensor_copy if b == 3 or (b == 2 and nxt % 4 == 0) else nc.scalar.copy)
+                    group_bank(nxt, b, nc.vector.tensor_copy if b == 3 else nc.scalar.copy)
                 mend_sq(nxt)
             group_sq(i, nc.scalar.copy)
             for step in steps[2:4]:

@@ -53,6 +53,7 @@ def tile_bgnna_kernel(tc, x, edge_index, weight, bias, out):
                 nc.sync.dma_start(out=e_t[:, w * k : w * k + w], in_=edge_index[t * P : (t + 1) * P, w * k : w * k + w])
 
         load(0, 4)
+        load(1, 1)
         x_sb = const.tile([P, N], BF16)
         nc.sync.dma_start(
             out=x_sb[:].rearrange("q (g r) -> q g r", g=NG),
@@ -60,7 +61,6 @@ def tile_bgnna_kernel(tc, x, edge_index, weight, bias, out):
         )
         w_sb = const.tile([P, C], BF16)
         nc.sync.dma_start(out=w_sb[:], in_=weight)
-        load(1, 1)
         diag_b = const.tile([P, NT], BF16)
         with nc.allow_non_contiguous_dma(reason="the 4096 diagonal elements, one each"):
             nc.sync.dma_start(
@@ -343,7 +343,7 @@ def tile_bgnna_kernel(tc, x, edge_index, weight, bias, out):
             stt = nc.vector.scalar_tensor_tensor
 
             def gram_sums():
-                gt = slice(2 * GRAM_TILES[0], 2 * hi, 2 * GRAM_STEP)
+                gt = slice(2 * GRAM_TILES[0], 2 * GRAM_TILES[-1] + 1, 2 * GRAM_STEP)
                 nc.vector.tensor_copy(out=sq_sums[:, gt], in_=folded[lo][:, NT : NT + len(GRAM_TILES)])
 
             sums = [
@@ -371,34 +371,35 @@ def tile_bgnna_kernel(tc, x, edge_index, weight, bias, out):
 
         more_loads(0)
         add_identity(0)
+        square_first(0)
         build_fold()
         transposes(0)
         new_grouped(0)
         for b in range(4):
-            group_bank(0, b, nc.vector.tensor_copy if b % 2 == 0 else nc.scalar.copy)
-        square_first(0)
+            group_bank(0, b, nc.vector.tensor_copy if b < 3 else nc.scalar.copy)
         squares(0)
-        row_sums(0)
-        x_transposed()
-        new_codes(0)
-        quantise(0, 0)
-        xw_grouped()
         add_identity(1)
         transposes(1)
+        new_codes(0)
+        quantise(0, 0)
         new_grouped(1)
         for b in range(4):
-            group_bank(1, b, nc.vector.tensor_copy if b in V_SLOTS else nc.scalar.copy)
+            group_bank(1, b, nc.vector.tensor_copy if b == 3 else nc.scalar.copy)
+        square_first(1)
+        squares(1)
+        x_transposed()
+        xw_grouped()
         diagonal_terms()
         mend_sq(0)
         sq_transposes(0)
+        mend_sq(1)
         add_identity(2)
+        row_sums(0)
         transposes(2)
         group_sq(0, nc.scalar.copy)
-        square_first(1)
         xw_quantised(0)
         quantise(0, 1)
         xw_quantised(1)
-        mend_sq(1)
         sq_transposes(1)
         add_identity(3)
         add_identity(4)
@@ -414,14 +415,15 @@ def tile_bgnna_kernel(tc, x, edge_index, weight, bias, out):
                 fold_sums(ROUND_1, NT)
             mx(i - 1, 0)
             mx(i - 1, 1)
-            squares(i)
+            if i > 1:
+                squares(i)
             for step in steps[0:2]:
                 step()
             if nxt < NT:
                 row_sums(i)
                 new_grouped(nxt)
                 for b in range(4):
-                    group_bank(nxt, b, nc.vector.tensor_copy if b == 3 else nc.scalar.copy)
+                    group_bank(nxt, b, nc.vector.tensor_copy if b == 3 or (b == 2 and nxt % 8 == 0) else nc.scalar.copy)
                 mend_sq(nxt)
             group_sq(i, nc.scalar.copy)
             for step in steps[2:4]:

@@ -83,6 +83,9 @@ def tile_bgnna_kernel(tc, x, edge_index, weight, bias, out):
         ones_b = const.tile([P, 2], BF16)
         nc.vector.memset(ones_b[:], 1.0)
 
+        warm = const.tile([P, 2], F32)
+        nc.scalar.activation(out=warm[:, 0:1], in_=ones_b[:, 0:1], func=ACT.Square)
+
         def build_fold():
             quarter = const.tile([P, 32], F32)
             nc.vector.tensor_reduce(out=quarter[:], in_=ident_f[:].rearrange("p (c t) -> p c t", t=4), axis=AX.X, op=ALU.add)
@@ -371,12 +374,12 @@ def tile_bgnna_kernel(tc, x, edge_index, weight, bias, out):
 
         more_loads(0)
         add_identity(0)
-        square_first(0)
         build_fold()
         transposes(0)
         new_grouped(0)
         for b in range(4):
-            group_bank(0, b, nc.vector.tensor_copy if b < 3 else nc.scalar.copy)
+            group_bank(0, b, nc.vector.tensor_copy if b % 2 == 0 else nc.scalar.copy)
+        square_first(0)
         squares(0)
         add_identity(1)
         transposes(1)
@@ -428,11 +431,11 @@ def tile_bgnna_kernel(tc, x, edge_index, weight, bias, out):
             group_sq(i, nc.scalar.copy)
             for step in steps[2:4]:
                 step()
-            if i % 2 == 0:
-                square_s(i - 2, i)
             if i + 2 < NT:
                 transposes(i + 2)
                 square_first(i + 2)
+            if i % 2 == 0:
+                square_s(i - 2, i)
             if nxt < NT:
                 sq_transposes(nxt)
             if i in GRAM_TILES:

@@ -20,13 +20,16 @@ PASS = 512
 NG = N // PASS
 BANK = 512
 HALF = N // 2
+PAIR = PASS // 2
 FLOPS = 2 * N * N * C * 2 + 2 * N * C * C
 
 GRAM_STEP = 5
-GRAM_TILES = (2, 7, 12, 17, 22)
+GRAM_TILES = (3, 8, 13, 18, 23)
 E_BUFS = 7
-V_SLOTS = (3,)
+AHEAD = 4
+SECOND_BANK = 8
 ROUND_1 = NT - 8
+FINISH = 6
 
 
 def tile_bgnna_kernel(tc, x, edge_index, weight, bias, out):
@@ -53,7 +56,7 @@ def tile_bgnna_kernel(tc, x, edge_index, weight, bias, out):
                 nc.sync.dma_start(out=e_t[:, w * k : w * k + w], in_=edge_index[t * P : (t + 1) * P, w * k : w * k + w])
 
         load(0, 4)
-        load(1, 1)
+        load(1, 2)
         x_sb = const.tile([P, N], BF16)
         nc.sync.dma_start(
             out=x_sb[:].rearrange("q (g r) -> q g r", g=NG),
@@ -159,37 +162,37 @@ def tile_bgnna_kernel(tc, x, edge_index, weight, bias, out):
 
         def transpose_pass(out_ap, words, w0):
             for u in range(2):
-                nc.tensor.transpose(out=out_ap[:, P * u : P * u + P], in_=words[:, w0 + u : w0 + 256 : 2], identity=ident_f[:])
+                nc.tensor.transpose(out=out_ap[:, P * u : P * u + P], in_=words[:, w0 + u : w0 + PAIR : 2], identity=ident_f[:])
 
-        def transposes(t, which_banks=(0, 1, 2, 3)):
+        def transposes(t):
             words = e_tiles[t][:].bitcast(F32)
             order = passes(t)
-            for b in which_banks:
+            for b in range(4):
                 tp = tpsum.tile([P, BANK], F32, tag="tp")
                 banks[(t, b)] = tp
                 for j in range(2):
-                    transpose_pass(tp[:, 256 * j : 256 * j + 256], words, 256 * order[2 * b + j])
+                    transpose_pass(tp[:, PAIR * j : PAIR * j + PAIR], words, PAIR * order[2 * b + j])
 
         def sq_transposes(t):
             tp = opsum.tile([P, BANK], F32, tag="op")
             sq_banks[t] = tp
-            transpose_pass(tp[:, 0:256], sq_nat[t][:].bitcast(F32), 256 * (t // 4 % (NG // 2)))
+            transpose_pass(tp[:, 0:PAIR], sq_nat[t][:].bitcast(F32), PAIR * (t // 4 % (NG // 2)))
 
         def new_grouped(t):
             adj_g = gpool.tile([P, N], BF16, name="adj_g", align_bytes=64)
             sq_g = gpool.tile([P, N], BF16, name="sq_g", align_bytes=64)
             grouped[t] = (adj_g, sq_g)
 
-        def group_bank(t, b, engine_copy):
-            engine_copy(
+        def group_bank(t, b, by_vector):
+            (nc.vector.tensor_copy if by_vector else nc.scalar.copy)(
                 out=grouped[t][0][:].bitcast(F32)[:, BANK * b : BANK * b + BANK].rearrange("p (g i u) -> p g i u", g=2, i=P, u=2),
                 in_=banks[(t, b)][:].rearrange("p (g u i) -> p g i u", g=2, u=2, i=P),
             )
 
-        def group_sq(t, engine_copy):
-            engine_copy(
-                out=grouped[t][1][:].bitcast(F32)[:, 0:256].rearrange("p (i u) -> p i u", i=P, u=2),
-                in_=sq_banks[t][:, 0:256].rearrange("p (u i) -> p i u", u=2, i=P),
+        def group_sq(t):
+            nc.scalar.copy(
+                out=grouped[t][1][:].bitcast(F32)[:, 0:PAIR].rearrange("p (i u) -> p i u", i=P, u=2),
+                in_=sq_banks[t][:, 0:PAIR].rearrange("p (u i) -> p i u", u=2, i=P),
             )
 
         def squares(t):
@@ -216,13 +219,11 @@ def tile_bgnna_kernel(tc, x, edge_index, weight, bias, out):
                         out=row_part[:, 4 * t + s : 4 * t + s + 1], lhsT=adj_g[:, c0 : c0 + P], rhs=ones_b[:, 0:1], start=(g == 0), stop=(g == NG - 1)
                     )
 
-        def gram(t, groups):
+        def gram(t):
             adj_g = grouped[t][0]
-            if t not in grams:
-                gr = opsum.tile([P, BANK], F32, tag="op")
-                grams[t] = gr
-            gr = grams[t]
-            for s in groups:
+            gr = opsum.tile([P, BANK], F32, tag="op")
+            grams[t] = gr
+            for s in range(4):
                 for g in range(NG):
                     c0 = PASS * g + P * s
                     nc.tensor.matmul(
@@ -230,23 +231,21 @@ def tile_bgnna_kernel(tc, x, edge_index, weight, bias, out):
                     )
 
         def gram_diagonal(t):
-            kept = work.tile([P, BANK], F32, name="kept")
-            nc.vector.tensor_tensor(
-                out=kept[:].rearrange("p (s m) -> p s m", s=4),
-                in0=grams[t][:].rearrange("p (s m) -> p s m", s=4),
-                in1=ident_f[:].unsqueeze(1).to_broadcast([P, 4, P]),
-                op=ALU.mult,
-            )
             at = 4 * GRAM_TILES.index(t)
-            nc.vector.tensor_reduce(out=gram_part[:, at : at + 4], in_=kept[:].rearrange("p (s m) -> p s m", s=4), axis=AX.X, op=ALU.add)
+            for s in range(4):
+                kept = work.tile([P, P], F32, name="kept")
+                nc.vector.scalar_tensor_tensor(
+                    out=kept[:], in0=grams[t][:, P * s : P * s + P], scalar=1.0, in1=ident_f[:], op0=ALU.mult, op1=ALU.mult,
+                    accum_out=gram_part[:, at + s : at + s + 1],
+                )
 
         xw_codes = []
 
         def mx(t, which):
-            if t == NT - 1 and t not in products:
+            if which == 0 and t == NT - 1:
                 sq_ps = opsum.tile([P, 2, 2, P], F32, tag="op")
                 products[t] = sq_ps
-            elif t not in products:
+            elif which == 0 and t % 2 == 0:
                 sq_ps = apsum.tile([P, 2, 2, P], F32, name="sq_ps")
                 products[t] = products[t + 1] = sq_ps
             l_c, l_s = codes[t][which]
@@ -287,7 +286,7 @@ def tile_bgnna_kernel(tc, x, edge_index, weight, bias, out):
                 for j in range(8):
                     b = 8 * k + j
                     nc.tensor.transpose(out=xtp[:, P * j : P * j + P], in_=x_sb[:, P * b : P * b + P], identity=ident_b[:])
-                (nc.vector.tensor_copy if k % 2 == 0 else nc.scalar.copy)(out=xt_sb[:, 1024 * k : 1024 * k + 1024], in_=xtp[:])
+                (nc.vector.tensor_copy if k == 2 else nc.scalar.copy)(out=xt_sb[:, 1024 * k : 1024 * k + 1024], in_=xtp[:])
 
         def xw_grouped():
             for g in range(NG):
@@ -351,8 +350,8 @@ def tile_bgnna_kernel(tc, x, edge_index, weight, bias, out):
 
             sums = [
                 lambda: tt(out=sm["rows"], in0=folded[lo][:, lo:hi], in1=sm["rest"], op=ALU.add),
-                lambda: tt(out=sm["ss_a"], in0=sq_sums[:, 2 * lo : 2 * hi : 2], in1=sq_sums[:, 2 * lo + 1 : 2 * hi : 2], op=ALU.add),
                 lambda: tt(out=sm["rows2"], in0=sm["rows"], in1=sm["rows"], op=ALU.mult),
+                lambda: tt(out=sm["ss_a"], in0=sq_sums[:, 2 * lo : 2 * hi : 2], in1=sq_sums[:, 2 * lo + 1 : 2 * hi : 2], op=ALU.add),
                 lambda: tt(out=sm["ss_b"], in0=sm["ss_a"], in1=sm["extra"], op=ALU.add),
                 lambda: tt(out=sm["den"], in0=sm["rows2"], in1=sm["ss_b"], op=ALU.subtract),
                 lambda: stt(out=sm["safe"], in0=sm["den"], scalar=0.0, in1=sm["den"], op0=ALU.is_equal, op1=ALU.add),
@@ -378,28 +377,28 @@ def tile_bgnna_kernel(tc, x, edge_index, weight, bias, out):
         transposes(0)
         new_grouped(0)
         for b in range(4):
-            group_bank(0, b, nc.vector.tensor_copy if b % 2 == 0 else nc.scalar.copy)
+            group_bank(0, b, b % 2 == 0)
         square_first(0)
-        squares(0)
         add_identity(1)
         transposes(1)
+        squares(0)
         new_codes(0)
         quantise(0, 0)
         new_grouped(1)
         for b in range(4):
-            group_bank(1, b, nc.vector.tensor_copy if b == 3 else nc.scalar.copy)
+            group_bank(1, b, b == 3)
         square_first(1)
         squares(1)
         x_transposed()
-        xw_grouped()
         diagonal_terms()
         mend_sq(0)
-        sq_transposes(0)
         mend_sq(1)
         add_identity(2)
+        xw_grouped()
+        sq_transposes(0)
         row_sums(0)
         transposes(2)
-        group_sq(0, nc.scalar.copy)
+        group_sq(0)
         xw_quantised(0)
         quantise(0, 1)
         xw_quantised(1)
@@ -410,9 +409,20 @@ def tile_bgnna_kernel(tc, x, edge_index, weight, bias, out):
         square_second(1)
         more_loads(2)
 
+        pending = []
+
+        def norm_step():
+            if pending:
+                pending.pop(0)()
+
         for i in range(1, NT):
             nxt = i + 1
-            steps = norm_steps(0, ROUND_1) if i == ROUND_1 + 3 else norm_steps(ROUND_1, NT) if i == NT - 1 else []
+            if i == NT - 5:
+                pending.extend(norm_steps(0, ROUND_1))
+            if i == NT - 1:
+                pending.extend(norm_steps(ROUND_1, NT))
+            if i == NT - 6:
+                fold_sums(0, ROUND_1)
             if i == NT - 1:
                 row_sums(i)
                 fold_sums(ROUND_1, NT)
@@ -420,17 +430,15 @@ def tile_bgnna_kernel(tc, x, edge_index, weight, bias, out):
             mx(i - 1, 1)
             if i > 1:
                 squares(i)
-            for step in steps[0:2]:
-                step()
+            norm_step()
             if nxt < NT:
                 row_sums(i)
                 new_grouped(nxt)
                 for b in range(4):
-                    group_bank(nxt, b, nc.vector.tensor_copy if b == 3 or (b == 2 and nxt % 8 == 0) else nc.scalar.copy)
+                    group_bank(nxt, b, b == 3 or (b == 2 and nxt % SECOND_BANK == 0))
                 mend_sq(nxt)
-            group_sq(i, nc.scalar.copy)
-            for step in steps[2:4]:
-                step()
+            norm_step()
+            group_sq(i)
             if i + 2 < NT:
                 transposes(i + 2)
                 square_first(i + 2)
@@ -439,41 +447,40 @@ def tile_bgnna_kernel(tc, x, edge_index, weight, bias, out):
             if nxt < NT:
                 sq_transposes(nxt)
             if i in GRAM_TILES:
-                gram(i, range(4))
+                gram(i)
             if i == NT - 1:
                 square_s(NT - 2, NT - 1)
-            if i == ROUND_1 + 2:
-                fold_sums(0, ROUND_1)
             new_codes(i)
             quantise(i, 0)
             if i - 1 in GRAM_TILES:
                 gram_diagonal(i - 1)
-            for step in steps[4:6]:
-                step()
-            if i + 4 < NT:
-                add_identity(i + 4)
+            norm_step()
+            if i + AHEAD < NT:
+                add_identity(i + AHEAD)
+                norm_step()
             square_second(len(second) if i >= NT - 2 else (len(second) * nxt) // NT)
-            if i > ROUND_1 + 3:
-                for t in range(6 * (i - ROUND_1 - 4), 6 * (i - ROUND_1 - 3)):
+            done = FINISH * (i - (NT - 4))
+            if done >= 0:
+                for t in range(done, done + FINISH):
                     finish(t)
+                    norm_step()
                 if i % 2 == 1:
-                    store(6 * (i - ROUND_1 - 5), 6 * (i - ROUND_1 - 3))
+                    store(done - FINISH, done + FINISH)
             quantise(i, 1)
-            for step in steps[6:7]:
-                step()
+            norm_step()
             if i % 2 == 0:
                 minus_q(i - 2, i)
-            for step in steps[7:]:
-                step()
+            norm_step()
             more_loads(i + 2)
 
         mx(NT - 1, 0)
         mx(NT - 1, 1)
         square_s(NT - 1, NT)
         minus_q(NT - 2, NT - 1)
-        for t in range(ROUND_1, NT - 1):
-            finish(t)
-        store(ROUND_1, NT - 1)
+        for lo, hi in ((ROUND_1, NT - 4), (NT - 4, NT - 1)):
+            for t in range(lo, hi):
+                finish(t)
+            store(lo, hi)
         minus_q(NT - 1, NT)
         finish(NT - 1)
         store(NT - 1, NT)

from contextlib import ExitStack

import concourse.mybir as mybir
from concourse.masks import make_identity

F32 = mybir.dt.float32
BF16 = mybir.dt.bfloat16
U32 = mybir.dt.uint32
U8 = mybir.dt.uint8
FP8X4 = mybir.dt.float8_e4m3fn_x4
ALU = mybir.AluOpType
ACT = mybir.ActivationFunctionType
AX = mybir.AxisListType

P = 128
N = 4096
C = 128
NT = N // P
PASS = 512
NG = N // PASS
BANK = 512
HALF = N // 2
PAIR = PASS // 2
FLOPS = 2 * N * N * C * 2 + 2 * N * C * C

GRAM_STEP = 5
GRAM_TILES = (3, 8, 13, 18, 23)
E_BUFS = 7
AHEAD = 4
SECOND_BANK = 8
ROUND_1 = NT - 8
FINISH = 6


def tile_bgnna_kernel(tc, x, edge_index, weight, bias, out):
    nc = tc.nc
    with ExitStack() as ctx:
        const = ctx.enter_context(tc.tile_pool(name="const", bufs=1))
        epool = ctx.enter_context(tc.tile_pool(name="epool", bufs=E_BUFS))
        gpool = ctx.enter_context(tc.tile_pool(name="gpool", bufs=3))
        cpool = ctx.enter_context(tc.tile_pool(name="cpool", bufs=3))
        work = ctx.enter_context(tc.tile_pool(name="work", bufs=2))
        spool = ctx.enter_context(tc.tile_pool(name="spool", bufs=3))
        tpsum = ctx.enter_context(tc.psum_pool(name="tpsum", bufs=4))
        opsum = ctx.enter_context(tc.psum_pool(name="opsum", bufs=2))
        apsum = ctx.enter_context(tc.psum_pool(name="apsum", bufs=1))
        ctx.enter_context(tc.manual_schedule())

        e_tiles = {}

        def load(t, pieces):
            e_t = epool.tile([P, N], BF16, name="e_t")
            e_tiles[t] = e_t
            w = N // pieces
            for k in range(pieces):
                nc.sync.dma_start(out=e_t[:, w * k : w * k + w], in_=edge_index[t * P : (t + 1) * P, w * k : w * k + w])

        load(0, 4)
        load(1, 2)
        x_sb = const.tile([P, N], BF16)
        nc.sync.dma_start(
            out=x_sb[:].rearrange("q (g r) -> q g r", g=NG),
            in_=x.rearrange("(g q t) i -> q g (t i)", g=NG, q=P, t=4),
        )
        w_sb = const.tile([P, C], BF16)
        nc.sync.dma_start(out=w_sb[:], in_=weight)
        diag_b = const.tile([P, NT], BF16)
        with nc.allow_non_contiguous_dma(reason="the 4096 diagonal elements, one each"):
            nc.sync.dma_start(
                out=diag_b[:],
                in_=edge_index.rearrange("a b -> (a b)")[0 : N * N : N + 1].rearrange("(t p) -> p t", p=P),
            )
        load(2, 1)
        load(3, 1)
        bias_bc = const.tile([P, C], BF16)
        nc.sync.dma_start(out=bias_bc[:], in_=bias.partition_broadcast(P))

        ident_f = const.tile([P, P], F32)
        make_identity(nc, ident_f[:])
        sq_sums = const.tile([P, 2 * NT], F32)
        nc.gpsimd.memset(sq_sums[:], 0.0)
        fold = const.tile([P, 4, P], F32)
        nc.gpsimd.memset(fold[:], 0.0)
        ident_b = const.tile([P, P], BF16)
        nc.vector.tensor_copy(out=ident_b[:], in_=ident_f[:])
        ones_b = const.tile([P, 2], BF16)
        nc.vector.memset(ones_b[:], 1.0)

        warm = const.tile([P, 2], F32)
        nc.scalar.activation(out=warm[:, 0:1], in_=ones_b[:, 0:1], func=ACT.Square)

        def build_fold():
            quarter = const.tile([P, 32], F32)
            nc.vector.tensor_reduce(out=quarter[:], in_=ident_f[:].rearrange("p (c t) -> p c t", t=4), axis=AX.X, op=ALU.add)
            for s in range(4):
                nc.vector.tensor_copy(out=fold[:, s, 32 * s : 32 * s + 32], in_=quarter[:])

        scrap = const.tile([P, HALF], BF16)
        result = const.tile([P, NT * C], F32)
        row_part = apsum.tile([P, 4 * NT], F32)
        gram_part = const.tile([P, 4 * len(GRAM_TILES)], F32)
        banks = {}
        grouped = {}
        sq_nat = {}
        sq_banks = {}
        codes = {}
        grams = {}
        products = {}
        squared = {}

        second = [t for t in range(NT) if t not in GRAM_TILES]
        progress = {"second": 0, "loads": 4}

        def d_half(t):
            return t // 4 // (NG // 2)

        def square_half(t, half, out_ap):
            cols = slice(HALF * half, HALF * half + HALF)
            nc.scalar.activation(
                out=out_ap, in_=e_tiles[t][:, cols], func=ACT.Square, accum_out=sq_sums[:, 2 * t + half : 2 * t + half + 1]
            )

        def square_first(t):
            sq_n = spool.tile([P, HALF], BF16, name="sq_n")
            sq_nat[t] = sq_n
            if t in GRAM_TILES:
                at = PASS * (t // 4 % (NG // 2))
                e_d = e_tiles[t][:, PASS * (t // 4) : PASS * (t // 4) + PASS]
                nc.vector.tensor_tensor(out=sq_n[:, at : at + PASS], in0=e_d, in1=e_d, op=ALU.mult)
            else:
                square_half(t, d_half(t), sq_n[:])

        def square_second(upto):
            while progress["second"] < upto:
                t = second[progress["second"]]
                square_half(t, 1 - d_half(t), scrap[:])
                progress["second"] += 1

        def more_loads(done):
            while progress["loads"] < NT:
                old = progress["loads"] - E_BUFS
                if old > done:
                    return
                if old >= 0 and old not in GRAM_TILES and second.index(old) >= progress["second"]:
                    return
                load(progress["loads"], 1)
                progress["loads"] += 1

        def add_identity(t):
            blk = e_tiles[t][:, P * t : P * t + P]
            nc.vector.tensor_tensor(out=blk, in0=blk, in1=ident_b[:], op=ALU.add)

        def mend_sq(t):
            at = PASS * (t // 4 % (NG // 2)) + P * (t % 4)
            blk = sq_nat[t][:, at : at + P]
            nc.vector.scalar_tensor_tensor(
                out=blk, in0=ident_b[:], scalar=small["mend"][:, t : t + 1], in1=blk, op0=ALU.mult, op1=ALU.add
            )

        def passes(t):
            return [t // 4] + [g for g in range(NG) if g != t // 4]

        def transpose_pass(out_ap, words, w0):
            for u in range(2):
                nc.tensor.transpose(out=out_ap[:, P * u : P * u + P], in_=words[:, w0 + u : w0 + PAIR : 2], identity=ident_f[:])

        def transposes(t):
            words = e_tiles[t][:].bitcast(F32)
            order = passes(t)
            for b in range(4):
                tp = tpsum.tile([P, BANK], F32, tag="tp")
                banks[(t, b)] = tp
                for j in range(2):
                    transpose_pass(tp[:, PAIR * j : PAIR * j + PAIR], words, PAIR * order[2 * b + j])

        def sq_transposes(t):
            tp = opsum.tile([P, BANK], F32, tag="op")
            sq_banks[t] = tp
            transpose_pass(tp[:, 0:PAIR], sq_nat[t][:].bitcast(F32), PAIR * (t // 4 % (NG // 2)))

        def new_grouped(t):
            adj_g = gpool.tile([P, N], BF16, name="adj_g", align_bytes=64)
            sq_g = gpool.tile([P, N], BF16, name="sq_g", align_bytes=64)
            grouped[t] = (adj_g, sq_g)

        def group_bank(t, b, by_vector):
            (nc.vector.tensor_copy if by_vector else nc.scalar.copy)(
                out=grouped[t][0][:].bitcast(F32)[:, BANK * b : BANK * b + BANK].rearrange("p (g i u) -> p g i u", g=2, i=P, u=2),
                in_=banks[(t, b)][:].rearrange("p (g u i) -> p g i u", g=2, u=2, i=P),
            )

        def group_sq(t):
            nc.scalar.copy(
                out=grouped[t][1][:].bitcast(F32)[:, 0:PAIR].rearrange("p (i u) -> p i u", i=P, u=2),
                in_=sq_banks[t][:, 0:PAIR].rearrange("p (u i) -> p i u", u=2, i=P),
            )

        def squares(t):
            adj_g, sq_g = grouped[t]
            nc.vector.tensor_tensor(out=sq_g[:, PASS:N], in0=adj_g[:, PASS:N], in1=adj_g[:, PASS:N], op=ALU.mult)

        def new_codes(t):
            a_c = cpool.tile([P, N // 4], U32, name="a_c", align_bytes=64)
            a_s = cpool.tile([P, N // 4], U8, name="a_s", align_bytes=64)
            s_c = cpool.tile([P, N // 4], U32, name="s_c", align_bytes=64)
            s_s = cpool.tile([P, N // 4], U8, name="s_s", align_bytes=64)
            codes[t] = ((a_c, a_s), (s_c, s_s))

        def quantise(t, which):
            words, scales = codes[t][which]
            nc.vector.quantize_mx(out=words[:].bitcast(FP8X4), scales=scales[:], in_=grouped[t][which][:])

        def row_sums(t):
            adj_g = grouped[t][0]
            for s in range(4):
                for g in range(NG):
                    c0 = PASS * g + P * s
                    nc.tensor.matmul(
                        out=row_part[:, 4 * t + s : 4 * t + s + 1], lhsT=adj_g[:, c0 : c0 + P], rhs=ones_b[:, 0:1], start=(g == 0), stop=(g == NG - 1)
                    )

        def gram(t):
            adj_g = grouped[t][0]
            gr = opsum.tile([P, BANK], F32, tag="op")
            grams[t] = gr
            for s in range(4):
                for g in range(NG):
                    c0 = PASS * g + P * s
                    nc.tensor.matmul(
                        out=gr[:, P * s : P * s + P], lhsT=adj_g[:, c0 : c0 + P], rhs=adj_g[:, c0 : c0 + P], start=(g == 0), stop=(g == NG - 1)
                    )

        def gram_diagonal(t):
            at = 4 * GRAM_TILES.index(t)
            for s in range(4):
                kept = work.tile([P, P], F32, name="kept")
                nc.vector.scalar_tensor_tensor(
                    out=kept[:], in0=grams[t][:, P * s : P * s + P], scalar=1.0, in1=ident_f[:], op0=ALU.mult, op1=ALU.mult,
                    accum_out=gram_part[:, at + s : at + s + 1],
                )

        xw_codes = []

        def mx(t, which):
            if which == 0 and t == NT - 1:
                sq_ps = opsum.tile([P, 2, 2, P], F32, tag="op")
                products[t] = sq_ps
            elif which == 0 and t % 2 == 0:
                sq_ps = apsum.tile([P, 2, 2, P], F32, name="sq_ps")
                products[t] = products[t + 1] = sq_ps
            l_c, l_s = codes[t][which]
            r_c, r_s = xw_codes[which]
            for slot, g in enumerate(passes(t)):
                lc = slice(P * slot, P * slot + P)
                rc = slice(P * g, P * g + P)
                nc.tensor.matmul_mx(
                    out=products[t][:, which, t % 2, :],
                    lhsT=l_c[:, lc].bitcast(FP8X4),
                    lhsT_scale=l_s[:, lc],
                    rhs=r_c[:, rc].bitcast(FP8X4),
                    rhs_scale=r_s[:, rc],
                    start=(slot == 0),
                    stop=(slot == NG - 1),
                )

        def square_s(lo, hi):
            s2 = work.tile([P, 2, P], F32, name="s2")
            squared[lo] = s2
            nc.scalar.activation(out=s2[:, 0 : hi - lo, :], in_=products[lo][:, 0, lo % 2 : lo % 2 + hi - lo, :], func=ACT.Square)

        def minus_q(lo, hi):
            nc.vector.tensor_tensor(
                out=result[:, C * lo : C * hi].rearrange("p (t c) -> p t c", c=C),
                in0=squared[lo][:, 0 : hi - lo, :],
                in1=products[lo][:, 1, lo % 2 : lo % 2 + hi - lo, :],
                op=ALU.subtract,
            )

        xt_sb = const.tile([P, N], BF16)
        xw_g = const.tile([P, N], BF16, align_bytes=64)
        xw2_g = const.tile([P, N], BF16, align_bytes=64)

        def x_transposed():
            for k in range(4):
                xtp = tpsum.tile([P, 2 * BANK], BF16, tag="tp")
                for j in range(8):
                    b = 8 * k + j
                    nc.tensor.transpose(out=xtp[:, P * j : P * j + P], in_=x_sb[:, P * b : P * b + P], identity=ident_b[:])
                (nc.vector.tensor_copy if k == 2 else nc.scalar.copy)(out=xt_sb[:, 1024 * k : 1024 * k + 1024], in_=xtp[:])

        def xw_grouped():
            for g in range(NG):
                xwp = tpsum.tile([P, BANK], F32, tag="tp")
                for t in range(4):
                    b = 4 * g + t
                    nc.tensor.matmul(out=xwp[:, P * t : P * t + P], lhsT=xt_sb[:, P * b : P * b + P], rhs=w_sb[:], start=True, stop=True)
                cols = slice(PASS * g, PASS * g + PASS)
                nc.vector.tensor_copy(out=xw_g[:, cols].rearrange("p (c t) -> p c t", t=4), in_=xwp[:].rearrange("p (t c) -> p c t", t=4))
                nc.scalar.activation(
                    out=xw2_g[:, cols].rearrange("p (c t) -> p c t", t=4), in_=xwp[:].rearrange("p (t c) -> p c t", t=4), func=ACT.Square
                )

        def xw_quantised(which):
            words = const.tile([P, N // 4], U32, name=("xw_c", "xw2_c")[which], align_bytes=64)
            scales = const.tile([P, N // 4], U8, name=("xw_s", "xw2_s")[which], align_bytes=64)
            xw_codes.append((words, scales))
            nc.vector.quantize_mx(out=words[:].bitcast(FP8X4), scales=scales[:], in_=(xw_g, xw2_g)[which][:])

        small = {}
        for name in ("diag", "one_d", "rest", "extra", "sq_x", "sq_r", "mend", "rows", "rows2", "ss_a", "ss_b", "den", "safe", "rec", "norm"):
            small[name] = const.tile([P, NT], F32, name=name)
        one_d_b = const.tile([P, NT], BF16)
        sq_x_b = const.tile([P, NT], BF16)
        sq_r_b = const.tile([P, NT], BF16)

        def diagonal_terms():
            nc.vector.tensor_copy(out=small["diag"][:], in_=diag_b[:])
            nc.vector.tensor_scalar_add(out=small["one_d"][:], in0=small["diag"][:], scalar1=1.0)
            nc.vector.tensor_copy(out=one_d_b[:], in_=small["one_d"][:])
            nc.vector.tensor_tensor(out=small["sq_x"][:], in0=small["one_d"][:], in1=small["one_d"][:], op=ALU.mult)
            nc.vector.tensor_tensor(out=small["sq_r"][:], in0=one_d_b[:], in1=one_d_b[:], op=ALU.mult)
            nc.vector.tensor_copy(out=sq_x_b[:], in_=small["sq_x"][:])
            nc.vector.tensor_copy(out=sq_r_b[:], in_=small["sq_r"][:])
            nc.vector.tensor_tensor(out=small["mend"][:], in0=sq_x_b[:], in1=sq_r_b[:], op=ALU.subtract)
            nc.vector.tensor_tensor(out=small["rest"][:], in0=small["one_d"][:], in1=one_d_b[:], op=ALU.subtract)
            nc.vector.tensor_tensor(out=small["extra"][:], in0=small["sq_x"][:], in1=small["sq_r"][:], op=ALU.subtract)

        row_sb = const.tile([P, 4 * NT], F32)
        folded = {}

        def fold_sums(lo, hi):
            nc.vector.tensor_copy(out=row_sb[:, 4 * lo : 4 * hi], in_=row_part[:, 4 * lo : 4 * hi])
            fo = opsum.tile([P, 2 * NT], F32, tag="op")
            folded[lo] = fo
            parts = [(row_sb[:, 4 * lo : 4 * hi], fo[:, lo:hi])]
            if lo == 0:
                parts.append((gram_part[:], fo[:, NT : NT + len(GRAM_TILES)]))
            for src, dst in parts:
                for s in range(4):
                    nc.tensor.matmul(out=dst, lhsT=fold[:, s, :], rhs=src.rearrange("p (t s) -> p s t", s=4)[:, s, :], start=(s == 0), stop=(s == 3))

        def norm_steps(lo, hi):
            sm = {name: tile[:, lo:hi] for name, tile in small.items()}
            tt = nc.vector.tensor_tensor
            stt = nc.vector.scalar_tensor_tensor

            def gram_sums():
                gt = slice(2 * GRAM_TILES[0], 2 * GRAM_TILES[-1] + 1, 2 * GRAM_STEP)
                nc.vector.tensor_copy(out=sq_sums[:, gt], in_=folded[lo][:, NT : NT + len(GRAM_TILES)])

            sums = [
                lambda: tt(out=sm["rows"], in0=folded[lo][:, lo:hi], in1=sm["rest"], op=ALU.add),
                lambda: tt(out=sm["rows2"], in0=sm["rows"], in1=sm["rows"], op=ALU.mult),
                lambda: tt(out=sm["ss_a"], in0=sq_sums[:, 2 * lo : 2 * hi : 2], in1=sq_sums[:, 2 * lo + 1 : 2 * hi : 2], op=ALU.add),
                lambda: tt(out=sm["ss_b"], in0=sm["ss_a"], in1=sm["extra"], op=ALU.add),
                lambda: tt(out=sm["den"], in0=sm["rows2"], in1=sm["ss_b"], op=ALU.subtract),
                lambda: stt(out=sm["safe"], in0=sm["den"], scalar=0.0, in1=sm["den"], op0=ALU.is_equal, op1=ALU.add),
                lambda: nc.vector.reciprocal(out=sm["rec"], in_=sm["safe"]),
                lambda: stt(out=sm["norm"], in0=sm["den"], scalar=0.0, in1=sm["rec"], op0=ALU.not_equal, op1=ALU.mult),
            ]
            return ([gram_sums] if lo == 0 else []) + sums

        out_tiles = out.rearrange("(t p) c -> p t c", p=P)

        def finish(t):
            cols = slice(C * t, C * t + C)
            nc.vector.scalar_tensor_tensor(
                out=result[:, cols], in0=result[:, cols], scalar=small["norm"][:, t : t + 1], in1=bias_bc[:], op0=ALU.mult, op1=ALU.add
            )

        def store(lo, hi):
            nc.sync.dma_start(out=out_tiles[:, lo:hi, :], in_=result[:, C * lo : C * hi].rearrange("p (t c) -> p t c", c=C))

        more_loads(0)
        add_identity(0)
        build_fold()
        transposes(0)
        new_grouped(0)
        for b in range(4):
            group_bank(0, b, b % 2 == 0)
        square_first(0)
        add_identity(1)
        transposes(1)
        squares(0)
        new_codes(0)
        quantise(0, 0)
        new_grouped(1)
        for b in range(4):
            group_bank(1, b, b == 3)
        square_first(1)
        squares(1)
        x_transposed()
        diagonal_terms()
        mend_sq(0)
        mend_sq(1)
        add_identity(2)
        xw_grouped()
        sq_transposes(0)
        row_sums(0)
        transposes(2)
        group_sq(0)
        xw_quantised(0)
        quantise(0, 1)
        xw_quantised(1)
        sq_transposes(1)
        add_identity(3)
        add_identity(4)
        square_first(2)
        square_second(1)
        more_loads(2)

        pending = []

        def norm_step():
            if pending:
                pending.pop(0)()

        for i in range(1, NT):
            nxt = i + 1
            if i == NT - 5:
                pending.extend(norm_steps(0, ROUND_1))
            if i == NT - 1:
                pending.extend(norm_steps(ROUND_1, NT))
            if i == NT - 6:
                fold_sums(0, ROUND_1)
            if i == NT - 1:
                row_sums(i)
                fold_sums(ROUND_1, NT)
            mx(i - 1, 0)
            mx(i - 1, 1)
            if i > 1:
                squares(i)
            norm_step()
            if nxt < NT:
                row_sums(i)
                new_grouped(nxt)
                for b in range(4):
                    group_bank(nxt, b, b == 3 or (b == 2 and nxt % SECOND_BANK == 0))
                mend_sq(nxt)
            norm_step()
            group_sq(i)
            if i + 2 < NT:
                transposes(i + 2)
                square_first(i + 2)
            if i % 2 == 0:
                square_s(i - 2, i)
            if nxt < NT:
                sq_transposes(nxt)
            if i in GRAM_TILES:
                gram(i)
            if i == NT - 1:
                square_s(NT - 2, NT - 1)
            new_codes(i)
            quantise(i, 0)
            if i - 1 in GRAM_TILES:
                gram_diagonal(i - 1)
            norm_step()
            if i + AHEAD < NT:
                add_identity(i + AHEAD)
                norm_step()
            square_second(len(second) if i >= NT - 2 else (len(second) * nxt) // NT)
            done = FINISH * (i - (NT - 4))
            if done >= 0:
                for t in range(done, done + FINISH):
                    finish(t)
                    norm_step()
                if i % 2 == 1:
                    store(done - FINISH, done + FINISH)
            quantise(i, 1)
            norm_step()
            if i % 2 == 0:
                minus_q(i - 2, i)
            norm_step()
            more_loads(i + 2)

        mx(NT - 1, 0)
        mx(NT - 1, 1)
        square_s(NT - 1, NT)
        minus_q(NT - 2, NT - 1)
        for lo, hi in ((ROUND_1, NT - 4), (NT - 4, NT - 1)):
            for t in range(lo, hi):
                finish(t)
            store(lo, hi)
        minus_q(NT - 1, NT)
        finish(NT - 1)
        store(NT - 1, NT)
